import numpy as np
import ml_dtypes


def mxq(x, axis, fmt="e4m3"):
    dtype, down = {"e4m3": (ml_dtypes.float8_e4m3fn, 7), "e5m2": (ml_dtypes.float8_e5m2, 14)}[fmt]
    v = np.moveaxis(np.asarray(x, np.float32).astype(ml_dtypes.bfloat16).astype(np.float64), axis, -1)
    blocks = v.reshape(v.shape[:-1] + (-1, 32))
    amax = np.abs(blocks).max(-1, keepdims=True)
    byte = np.maximum(np.where(amax > 0, np.frexp(amax)[1] - 1 + 127, 0) - down, 1)
    scale = np.exp2(byte - 127.0)
    codes = (blocks / scale).astype(np.float32).astype(dtype).astype(np.float64)
    return np.moveaxis((codes * scale).reshape(v.shape), -1, axis)


WIDE = False


def mx_kscale(k):
    if not WIDE:
        return np.ones(k)
    levels = np.array([10, -10, 5, -5, 0])
    a = np.random.permutation(np.resize(levels, k // 512 * 4)).reshape(k // 512, 4)
    idx = np.arange(k)
    return np.exp2(a[idx // 512, idx % 128 // 32])


BF16 = ml_dtypes.bfloat16


def bf(x):
    return np.asarray(x, np.float32).astype(BF16)


def f64(x):
    return np.asarray(x).astype(np.float64)


BATCH, SEQ, IN_F, OUT_F, GRID_SIZE = 4, 128, 1024, 1024, 8
GRID_LO, GRID_HI = -2.0, 2.0


def _grid_and_inv_denom():
    grid = np.linspace(GRID_LO, GRID_HI, GRID_SIZE)
    inv_denom = 1.0 / (float((GRID_HI - GRID_LO) / (GRID_SIZE - 1)) + 1e-06)
    return grid, inv_denom


def silu(v):
    e = np.exp(-np.abs(v))
    return v * np.where(v >= 0.0, 1.0, e) / (1.0 + e)


def setup_inputs():
    s = mx_kscale(IN_F)
    return {"x": bf(np.random.standard_normal((BATCH, SEQ, IN_F)) * s),
            "base_w": bf(np.random.standard_normal((OUT_F, IN_F)) / np.sqrt(IN_F) / s),
            "base_b": bf(np.random.standard_normal(OUT_F) * 0.1),
            "spline_w": bf(np.random.standard_normal((OUT_F, IN_F, GRID_SIZE)) * 0.64 / np.sqrt(IN_F))}


def reference(x, base_w, base_b, spline_w):
    grid, inv_denom = _grid_and_inv_denom()
    lead = x.shape[:-1]
    x_flat = f64(x).reshape(-1, IN_F)
    act = silu(x_flat)
    base_out = (mxq(act, 1, "e4m3") @ mxq(f64(base_w), 1, "e4m3").T) + f64(base_b)
    basis = np.exp(-(((x_flat[..., None] - grid) * inv_denom) ** 2))
    bq = mxq(basis.reshape(-1, IN_F * GRID_SIZE), 1, "e4m3")
    wq = mxq(f64(spline_w).reshape(OUT_F, IN_F * GRID_SIZE), 1, "e4m3")
    spline_out = bq @ wq.T
    out = base_out + spline_out
    return out.reshape(*lead, OUT_F)

@@ -1,0 +1,347 @@
+from contextlib import ExitStack
+
+import concourse.mybir as mybir
+from concourse.masks import make_identity
+
+F32 = mybir.dt.float32
+BF16 = mybir.dt.bfloat16
+U32 = mybir.dt.uint32
+U8 = mybir.dt.uint8
+FP8X4 = mybir.dt.float8_e4m3fn_x4
+ACT = mybir.ActivationFunctionType
+ALU = mybir.AluOpType
+AX = mybir.AxisListType
+
+P = 128
+ROWS = 512
+IN_F = 1024
+OUT_F = 1024
+GRID = 8
+HALF = 512
+RH = 256
+STEP = 4.0 / 7.0
+CINV = 1.0 / (STEP + 1e-06)
+CLAMP = 64.0
+
+FLOPS = 2 * ROWS * OUT_F * (IN_F + IN_F * GRID)
+
+PATH = {
+    (0, 0): "sel", (0, 1): "sel", (0, 2): "sel", (0, 3): "sel",
+    (1, 0): "exp", (1, 1): "exp", (1, 2): "exp", (1, 3): "exp",
+}
+
+
+def tile_kanlinear_kernel(tc, x, base_w, base_b, spline_w, out):
+    nc = tc.nc
+    xf = x.flatten_outer_dims()
+    of = out.flatten_outer_dims()
+    sw = spline_w.rearrange("o i g -> o (i g)")
+
+    with ExitStack() as ctx:
+        const = ctx.enter_context(tc.tile_pool(name="const", bufs=1))
+        keep = ctx.enter_context(tc.tile_pool(name="keep", bufs=1))
+        chunks = ctx.enter_context(tc.tile_pool(name="chunks", bufs=3))
+        wgrps = ctx.enter_context(tc.tile_pool(name="wgrps", bufs=3))
+        ypool = ctx.enter_context(tc.tile_pool(name="ypool", bufs=1))
+        ytp = ctx.enter_context(tc.tile_pool(name="ytp", bufs=3))
+        xtp = ctx.enter_context(tc.tile_pool(name="xtp", bufs=2))
+        qpool = ctx.enter_context(tc.tile_pool(name="qpool", bufs=2))
+        bgrps = ctx.enter_context(tc.tile_pool(name="bgrps", bufs=3))
+        bc0 = ctx.enter_context(tc.tile_pool(name="bc0", bufs=6))
+        bc1 = ctx.enter_context(tc.tile_pool(name="bc1", bufs=6))
+        ostage = ctx.enter_context(tc.tile_pool(name="ostage", bufs=3))
+        accp = ctx.enter_context(tc.psum_pool(name="accp", bufs=4))
+        wk = ctx.enter_context(tc.psum_pool(name="wk", bufs=4))
+
+        x_nat = keep.tile([P, 4 * IN_F], BF16)
+        nc.sync.dma_start(
+            out=x_nat[:].rearrange("p (m i) -> p m i", m=4),
+            in_=xf.rearrange("(m p) i -> p m i", p=P),
+        )
+        bias_bc = const.tile([P, OUT_F], BF16)
+        nc.gpsimd.dma_start(out=bias_bc[:], in_=base_b.partition_broadcast(P))
+
+        def load_chunk(i):
+            ch = chunks.tile([P, 8192], BF16, tag="chunk", name="chunk%d" % i)
+            if i == 0:
+                nc.sync.dma_start(
+                    out=ch[:].rearrange("p (n k) -> p n k", n=8),
+                    in_=base_w.rearrange("(n p) k -> p n k", p=P),
+                )
+            else:
+                h, half = divmod(i - 1, 2)
+                nc.sync.dma_start(
+                    out=ch[:].rearrange("p (n k) -> p n k", n=4),
+                    in_=sw[HALF * half : HALF * half + HALF, 2048 * h : 2048 * h + 2048].rearrange(
+                        "(n p) k -> p n k", p=P
+                    ),
+                )
+            return ch[:].bitcast(F32)
+
+        chunk_words = {}
+        for i in range(3):
+            chunk_words[i] = load_chunk(i)
+
+        ident_f = const.tile([P, P], F32)
+        make_identity(nc, ident_f[:])
+        ident_b = const.tile([P, P], BF16)
+        make_identity(nc, ident_b[:])
+        sel = const.tile([P, 4 * P], BF16)
+        for a in range(4):
+            nc.vector.tensor_copy(
+                out=sel[:, P * a : P * a + P].rearrange("p (f s) -> p f s", s=4),
+                in_=ident_b[:, 32 * a : 32 * a + 32].unsqueeze(2).to_broadcast([P, 32, 4]),
+            )
+        sq_bias = []
+        for e in range(2):
+            vals = const.tile([P, P], F32, name="vals%d" % e)
+            for q in range(4):
+                nc.vector.memset(vals[:].rearrange("p (f s) -> p f s", s=4)[:, :, q], float(2 * q + e))
+            nc.vector.tensor_tensor(out=vals[:], in0=vals[:], in1=ident_f[:], op=ALU.mult)
+            j_e = const.tile([P, 1], F32, name="grid_index%d" % e)
+            nc.vector.reduce_sum(out=j_e[:], in_=vals[:], axis=AX.X)
+            b_e = const.tile([P, 1], F32, name="sq_bias%d" % e)
+            nc.vector.tensor_scalar(
+                out=b_e[:], in0=j_e[:], scalar1=-CINV * STEP, scalar2=2.0 * CINV, op0=ALU.mult, op1=ALU.add
+            )
+            sq_bias.append(b_e)
+        fold = const.tile([P, 32], BF16)
+        fold2 = const.tile([P, 32], BF16)
+        nc.vector.tensor_tensor(out=fold[:], in0=ident_b[:, 0:32], in1=ident_b[:, 32:64], op=ALU.add)
+        nc.vector.tensor_tensor(out=fold2[:], in0=ident_b[:, 64:96], in1=ident_b[:, 96:128], op=ALU.add)
+        nc.vector.tensor_tensor(out=fold[:], in0=fold[:], in1=fold2[:], op=ALU.add)
+        coef = []
+        for e in range(2):
+            c_e = const.tile([P, P], BF16, name="coef%d" % e)
+            c_v = c_e[:].rearrange("p (f s) -> p f s", s=4)
+            nc.vector.memset(c_e[0:64, :], 49.0)
+            for q in range(4):
+                j = 2 * q + e
+                nc.vector.memset(c_v[64:96, :, q], float(196 - 56 * j))
+                nc.vector.memset(c_v[96:128, :, q], float((14 - 4 * j) * (14 - 4 * j)))
+            nc.vector.tensor_tensor(
+                out=c_v, in0=c_v, in1=fold[:].unsqueeze(2).to_broadcast([P, 32, 4]), op=ALU.mult
+            )
+            coef.append(c_e)
+        bias_f = const.tile([P, OUT_F], F32)
+        nc.vector.tensor_copy(out=bias_f[:], in_=bias_bc[:])
+
+        x_words = x_nat[:].bitcast(F32)
+
+        def quantise(pool, grp, nm):
+            codes = pool.tile([P, RH], U32, align_bytes=64, tag="codes", name="bq_" + nm)
+            plane = pool.tile([P, RH], U8, align_bytes=64, tag="plane", name="bs_" + nm)
+            nc.vector.quantize_mx(out=codes[:].bitcast(FP8X4), scales=plane[:], in_=grp[:])
+            return codes, plane
+
+        acts = {}
+        for r in range(2):
+            for g in range(2):
+                sp = wk.tile([P, 512], F32, tag="wk", name="sp")
+                for u in range(2):
+                    for mm in range(2):
+                        c0 = 512 * (2 * r + mm) + 256 * g + P * u
+                        nc.tensor.transpose(
+                            out=sp[:, 256 * u + P * mm : 256 * u + P * mm + P],
+                            in_=x_words[:, c0 : c0 + P],
+                            identity=ident_f[:],
+                        )
+                grp = bgrps.tile([P, 4 * RH], BF16, align_bytes=64, tag="bgrp", name="sgrp")
+                nc.scalar.activation(
+                    out=grp[:].rearrange("p (r u e) -> p r u e", u=2, e=2),
+                    in_=sp[:].bitcast(BF16).rearrange("p (u r e) -> p r u e", u=2, e=2),
+                    func=ACT.Silu,
+                )
+                codes = keep.tile([P, RH], U32, align_bytes=64, name="sq_%d_%d" % (r, g))
+                plane = keep.tile([P, RH], U8, align_bytes=64, name="ss_%d_%d" % (r, g))
+                nc.vector.quantize_mx(out=codes[:].bitcast(FP8X4), scales=plane[:], in_=grp[:])
+                acts[(("b", g), r)] = (codes, plane)
+
+        prepared = {}
+
+        def prep_set(r, h):
+            if PATH[(r, h)] == "sel":
+                xp = wk.tile([P, 512], BF16, tag="wk", name="xp")
+                for s in range(2):
+                    for mm in range(2):
+                        c0 = IN_F * (2 * r + mm) + P * (2 * h + s)
+                        nc.tensor.transpose(
+                            out=xp[:, 256 * s + P * mm : 256 * s + P * mm + P],
+                            in_=x_nat[:, c0 : c0 + P],
+                            identity=ident_b[:],
+                        )
+                xt = xtp.tile([P, 512], BF16, tag="xt", name="xt")
+                nc.vector.tensor_copy(out=xt[:], in_=xp[:])
+                prepared[(r, h)] = xt
+                return
+            y = ypool.tile([P, 2048], BF16, tag="y", name="y")
+            yv = y[:].rearrange("p (m j s f) -> p m j s f", m=2, j=8, s=4)
+            xs = x_nat[:].rearrange("p (m j f) -> p m j f", m=4, j=32)[:, 2 * r : 2 * r + 2, 8 * h : 8 * h + 8, :]
+            nc.gpsimd.tensor_scalar(
+                out=yv[:, :, :, 2, :], in0=xs, scalar1=CLAMP, scalar2=-CLAMP, op0=ALU.min, op1=ALU.max
+            )
+            sqr = ypool.tile([P, 512], F32, tag="sqr", name="sqr")
+            sv = sqr[:].rearrange("p (m j f) -> p m j f", m=2, j=8)
+            nc.gpsimd.tensor_tensor(out=sv, in0=yv[:, :, :, 2, :], in1=yv[:, :, :, 2, :], op=ALU.mult)
+            nc.gpsimd.tensor_tensor(out=yv[:, :, :, 0, :], in0=yv[:, :, :, 2, :], in1=yv[:, :, :, 2, :], op=ALU.mult)
+            nc.gpsimd.tensor_tensor(out=yv[:, :, :, 1, :], in0=sv, in1=yv[:, :, :, 0, :], op=ALU.subtract)
+            nc.gpsimd.memset(yv[:, :, :, 3, :], 1.0)
+            yt = ytp.tile([P, 2048], BF16, tag="yt", name="yt")
+            for jh in range(2):
+                yp = wk.tile([P, 1024], BF16, tag="wk", name="yp")
+                for j4 in range(4):
+                    for mm in range(2):
+                        c0 = 1024 * mm + P * (4 * jh + j4)
+                        nc.tensor.transpose(
+                            out=yp[:, 256 * j4 + P * mm : 256 * j4 + P * mm + P],
+                            in_=y[:, c0 : c0 + P],
+                            identity=ident_b[:],
+                        )
+                nc.vector.tensor_copy(out=yt[:, 1024 * jh : 1024 * jh + 1024], in_=yp[:])
+            prepared[(r, h)] = yt
+
+        def basis(c, r):
+            h, a = divmod(c, 4)
+            src = prepared[(r, h)]
+            grp = bgrps.tile([P, 4 * RH], BF16, align_bytes=64, tag="bgrp", name="bgrp")
+            if PATH[(r, h)] == "sel":
+                x4 = wk.tile([P, 512], F32, tag="wk", name="x4")
+                for u in range(2):
+                    nc.tensor.matmul(
+                        out=x4[:, RH * u : RH * u + RH],
+                        lhsT=sel[:, P * a : P * a + P],
+                        rhs=src[:, RH * u : RH * u + RH],
+                        start=True,
+                        stop=True,
+                    )
+                qq = qpool.tile([P, 4 * RH], F32, tag="qq", name="qq")
+                for e in range(2):
+                    nc.scalar.activation(
+                        out=qq[:].rearrange("p (u e r) -> p u e r", u=2, e=2)[:, :, e, :],
+                        in_=x4[:].rearrange("p (u r) -> p u r", u=2),
+                        func=ACT.Square,
+                        bias=sq_bias[e][:, 0:1],
+                        scale=CINV,
+                    )
+                nc.scalar.activation(
+                    out=grp[:].rearrange("p (r t) -> p r t", t=4),
+                    in_=qq[:].rearrange("p (t r) -> p r t", t=4),
+                    func=ACT.Exp,
+                    scale=-1.0,
+                )
+            else:
+                for mm in range(2):
+                    ex = wk.tile([P, 512], F32, tag="wk", name="ex")
+                    for u in range(2):
+                        for e in range(2):
+                            c0 = 256 * (a + 4 * u) + P * mm
+                            nc.tensor.matmul(
+                                out=ex[:, P * (2 * u + e) : P * (2 * u + e) + P],
+                                lhsT=coef[e][:],
+                                rhs=src[:, c0 : c0 + P],
+                                start=True,
+                                stop=True,
+                            )
+                    nc.scalar.activation(
+                        out=grp[:, 512 * mm : 512 * mm + 512].rearrange("p (r t) -> p r t", t=4),
+                        in_=ex[:].rearrange("p (t r) -> p r t", t=4),
+                        func=ACT.Exp,
+                        scale=-(CINV / 7.0) * (CINV / 7.0),
+                    )
+            acts[(("s", c), r)] = quantise(bc0 if r == 0 else bc1, grp, "%d_%d" % (c, r))
+
+        wts = {}
+        counter = [0]
+
+        def weights(kk, half, words, col_of):
+            wgrp = wgrps.tile([P, 4 * HALF], BF16, align_bytes=64, tag="wgrp", name="wgrp")
+            wgrp_w = wgrp[:].bitcast(F32)
+            for q in range(2):
+                wt = wk.tile([P, 512], F32, tag="wk", name="wt")
+                for nn in range(2):
+                    for u in range(2):
+                        c0 = col_of(2 * q + nn, u)
+                        nc.tensor.transpose(
+                            out=wt[:, 256 * nn + P * u : 256 * nn + P * u + P],
+                            in_=words[:, c0 : c0 + P],
+                            identity=ident_f[:],
+                        )
+                dst = wgrp_w[:, 512 * q : 512 * q + 512].rearrange("p (n o u) -> p n o u", n=2, u=2)
+                srcv = wt[:].rearrange("p (n u o) -> p n o u", n=2, u=2)
+                if q == 1 and counter[0] % 2 == 0:
+                    nc.scalar.copy(out=dst, in_=srcv)
+                else:
+                    nc.vector.tensor_copy(out=dst, in_=srcv)
+            counter[0] += 1
+            nm = "%s%d_%d" % (kk[0], kk[1], half)
+            codes = keep.tile([P, HALF], U32, align_bytes=64, name="wq_" + nm)
+            plane = keep.tile([P, HALF], U8, align_bytes=64, name="ws_" + nm)
+            nc.vector.quantize_mx(out=codes[:].bitcast(FP8X4), scales=plane[:], in_=wgrp[:])
+            wts[(kk, half)] = (codes, plane)
+
+        def mx(accs, kk, r, half):
+            a_c, a_p = acts[(kk, r)]
+            w_c, w_p = wts[(kk, half)]
+            for mm in range(2):
+                nc.tensor.matmul_mx(
+                    out=accs[(mm, half)][:],
+                    lhsT=a_c[:, P * mm : P * mm + P].bitcast(FP8X4),
+                    lhsT_scale=a_p[:, P * mm : P * mm + P],
+                    rhs=w_c[:].bitcast(FP8X4),
+                    rhs_scale=w_p[:],
+                    start=(kk == ("b", 0)),
+                    stop=(kk == ("s", 15)),
+                )
+
+        def new_accs():
+            accs = {}
+            for half in range(2):
+                for mm in range(2):
+                    accs[(mm, half)] = accp.tile([P, HALF], F32, tag="acc", name="acc%d%d" % (mm, half))
+            return accs
+
+        def finish(accs, r, half):
+            cols = slice(HALF * half, HALF * half + HALF)
+            for mm in range(2):
+                res = ostage.tile([P, HALF], F32, tag="res", name="res")
+                nc.vector.tensor_tensor(out=res[:], in0=accs[(mm, half)][:], in1=bias_f[:, cols], op=ALU.add)
+                r0 = RH * r + P * mm
+                nc.sync.dma_start(out=of[r0 : r0 + P, cols], in_=res[:])
+
+        accs = new_accs()
+        prep_set(0, 0)
+        for g in range(2):
+            for half in range(2):
+                weights(("b", g), half, chunk_words[0], lambda n, u: 512 * (4 * half + n) + 256 * g + P * u)
+                mx(accs, ("b", g), 0, half)
+        for h in range(4):
+            if h < 3:
+                prep_set(0, h + 1)
+                prep_set(1, h)
+            for half in range(2):
+                i = 1 + 2 * h + half
+                if i + 2 <= 8:
+                    chunk_words[i + 2] = load_chunk(i + 2)
+                for a in range(4):
+                    c = 4 * h + a
+                    if half == 0:
+                        basis(c, 0)
+                    weights(("s", c), half, chunk_words[i], lambda n, u: 1024 * n + P * a + 512 * u)
+                    mx(accs, ("s", c), 0, half)
+        for half in range(2):
+            finish(accs, 0, half)
+
+        accs = new_accs()
+        for g in range(2):
+            for half in range(2):
+                mx(accs, ("b", g), 1, half)
+        for h in range(4):
+            for a in range(4):
+                c = 4 * h + a
+                basis(c, 1)
+                for half in range(2):
+                    mx(accs, ("s", c), 1, half)
+            if h == 0:
+                prep_set(1, 3)
+        for half in range(2):
+            finish(accs, 1, half)

@@ -25,10 +25,11 @@ CLAMP = 64.0
 
 FLOPS = 2 * ROWS * OUT_F * (IN_F + IN_F * GRID)
 
-PATH = {
-    (0, 0): "sel", (0, 1): "sel", (0, 2): "sel", (0, 3): "sel",
-    (1, 0): "exp", (1, 1): "exp", (1, 2): "exp", (1, 3): "exp",
-}
+
+def act_evicts(s, b):
+    if b == 3:
+        return s >= 1 and (s <= 3 or s % 3 != 0)
+    return b == 1 and s in (1, 2)
 
 
 def tile_kanlinear_kernel(tc, x, base_w, base_b, spline_w, out):
@@ -36,38 +37,31 @@ def tile_kanlinear_kernel(tc, x, base_w, base_b, spline_w, out):
     xf = x.flatten_outer_dims()
     of = out.flatten_outer_dims()
     sw = spline_w.rearrange("o i g -> o (i g)")
+    scr = of[384:512, :].rearrange("(q a) (b w) -> q (a b) w", a=4, w=P)
 
     with ExitStack() as ctx:
+        ctx.enter_context(tc.manual_schedule())
         const = ctx.enter_context(tc.tile_pool(name="const", bufs=1))
         keep = ctx.enter_context(tc.tile_pool(name="keep", bufs=1))
         chunks = ctx.enter_context(tc.tile_pool(name="chunks", bufs=3))
         wgrps = ctx.enter_context(tc.tile_pool(name="wgrps", bufs=3))
-        ypool = ctx.enter_context(tc.tile_pool(name="ypool", bufs=1))
-        ytp = ctx.enter_context(tc.tile_pool(name="ytp", bufs=3))
-        xtp = ctx.enter_context(tc.tile_pool(name="xtp", bufs=2))
+        x4p = ctx.enter_context(tc.tile_pool(name="x4p", bufs=2))
         qpool = ctx.enter_context(tc.tile_pool(name="qpool", bufs=2))
         bgrps = ctx.enter_context(tc.tile_pool(name="bgrps", bufs=3))
-        bc0 = ctx.enter_context(tc.tile_pool(name="bc0", bufs=6))
-        bc1 = ctx.enter_context(tc.tile_pool(name="bc1", bufs=6))
-        ostage = ctx.enter_context(tc.tile_pool(name="ostage", bufs=3))
+        bcp = ctx.enter_context(tc.tile_pool(name="bcp", bufs=7))
         accp = ctx.enter_context(tc.psum_pool(name="accp", bufs=4))
         wk = ctx.enter_context(tc.psum_pool(name="wk", bufs=4))
 
-        x_nat = keep.tile([P, 4 * IN_F], BF16)
-        nc.sync.dma_start(
-            out=x_nat[:].rearrange("p (m i) -> p m i", m=4),
-            in_=xf.rearrange("(m p) i -> p m i", p=P),
-        )
-        bias_bc = const.tile([P, OUT_F], BF16)
-        nc.gpsimd.dma_start(out=bias_bc[:], in_=base_b.partition_broadcast(P))
+        chunk_words = {}
 
         def load_chunk(i):
             ch = chunks.tile([P, 8192], BF16, tag="chunk", name="chunk%d" % i)
             if i == 0:
-                nc.sync.dma_start(
-                    out=ch[:].rearrange("p (n k) -> p n k", n=8),
-                    in_=base_w.rearrange("(n p) k -> p n k", p=P),
-                )
+                for half in range(2):
+                    nc.sync.dma_start(
+                        out=ch[:, 4096 * half : 4096 * half + 4096].rearrange("p (n k) -> p n k", n=4),
+                        in_=base_w[HALF * half : HALF * half + HALF, :].rearrange("(n p) k -> p n k", p=P),
+                    )
             else:
                 h, half = divmod(i - 1, 2)
                 nc.sync.dma_start(
@@ -76,117 +70,208 @@ def tile_kanlinear_kernel(tc, x, base_w, base_b, spline_w, out):
                         "(n p) k -> p n k", p=P
                     ),
                 )
-            return ch[:].bitcast(F32)
+            chunk_words[i] = ch[:].bitcast(F32)
 
-        chunk_words = {}
-        for i in range(3):
-            chunk_words[i] = load_chunk(i)
+        x4s = {}
 
-        ident_f = const.tile([P, P], F32)
-        make_identity(nc, ident_f[:])
-        ident_b = const.tile([P, P], BF16)
-        make_identity(nc, ident_b[:])
-        sel = const.tile([P, 4 * P], BF16)
-        for a in range(4):
-            nc.vector.tensor_copy(
-                out=sel[:, P * a : P * a + P].rearrange("p (f s) -> p f s", s=4),
-                in_=ident_b[:, 32 * a : 32 * a + 32].unsqueeze(2).to_broadcast([P, 32, 4]),
-            )
-        sq_bias = []
-        for e in range(2):
-            vals = const.tile([P, P], F32, name="vals%d" % e)
-            for q in range(4):
-                nc.vector.memset(vals[:].rearrange("p (f s) -> p f s", s=4)[:, :, q], float(2 * q + e))
-            nc.vector.tensor_tensor(out=vals[:], in0=vals[:], in1=ident_f[:], op=ALU.mult)
-            j_e = const.tile([P, 1], F32, name="grid_index%d" % e)
-            nc.vector.reduce_sum(out=j_e[:], in_=vals[:], axis=AX.X)
-            b_e = const.tile([P, 1], F32, name="sq_bias%d" % e)
-            nc.vector.tensor_scalar(
-                out=b_e[:], in0=j_e[:], scalar1=-CINV * STEP, scalar2=2.0 * CINV, op0=ALU.mult, op1=ALU.add
-            )
-            sq_bias.append(b_e)
-        fold = const.tile([P, 32], BF16)
-        fold2 = const.tile([P, 32], BF16)
-        nc.vector.tensor_tensor(out=fold[:], in0=ident_b[:, 0:32], in1=ident_b[:, 32:64], op=ALU.add)
-        nc.vector.tensor_tensor(out=fold2[:], in0=ident_b[:, 64:96], in1=ident_b[:, 96:128], op=ALU.add)
-        nc.vector.tensor_tensor(out=fold[:], in0=fold[:], in1=fold2[:], op=ALU.add)
-        coef = []
-        for e in range(2):
-            c_e = const.tile([P, P], BF16, name="coef%d" % e)
-            c_v = c_e[:].rearrange("p (f s) -> p f s", s=4)
-            nc.vector.memset(c_e[0:64, :], 49.0)
-            for q in range(4):
-                j = 2 * q + e
-                nc.vector.memset(c_v[64:96, :, q], float(196 - 56 * j))
-                nc.vector.memset(c_v[96:128, :, q], float((14 - 4 * j) * (14 - 4 * j)))
-            nc.vector.tensor_tensor(
-                out=c_v, in0=c_v, in1=fold[:].unsqueeze(2).to_broadcast([P, 32, 4]), op=ALU.mult
-            )
-            coef.append(c_e)
-        bias_f = const.tile([P, OUT_F], F32)
-        nc.vector.tensor_copy(out=bias_f[:], in_=bias_bc[:])
-
-        x_words = x_nat[:].bitcast(F32)
-
-        def quantise(pool, grp, nm):
-            codes = pool.tile([P, RH], U32, align_bytes=64, tag="codes", name="bq_" + nm)
-            plane = pool.tile([P, RH], U8, align_bytes=64, tag="plane", name="bs_" + nm)
-            nc.vector.quantize_mx(out=codes[:].bitcast(FP8X4), scales=plane[:], in_=grp[:])
-            return codes, plane
+        def load_x4(h, queue):
+            t = x4p.tile([P, 2048], BF16, tag="x4", name="x4_%d" % h)
+            tw = t[:].bitcast(F32)
+            for s in range(4):
+                queue.dma_start(
+                    out=tw[s:P:4, :], in_=scr[:, 8 * h : 8 * h + 8, :].rearrange("q j w -> q (j w)")
+                )
+            x4s[h] = t
 
         acts = {}
-        for r in range(2):
-            for g in range(2):
-                sp = wk.tile([P, 512], F32, tag="wk", name="sp")
-                for u in range(2):
-                    for mm in range(2):
-                        c0 = 512 * (2 * r + mm) + 256 * g + P * u
-                        nc.tensor.transpose(
-                            out=sp[:, 256 * u + P * mm : 256 * u + P * mm + P],
-                            in_=x_words[:, c0 : c0 + P],
-                            identity=ident_f[:],
-                        )
-                grp = bgrps.tile([P, 4 * RH], BF16, align_bytes=64, tag="bgrp", name="sgrp")
-                nc.scalar.activation(
-                    out=grp[:].rearrange("p (r u e) -> p r u e", u=2, e=2),
-                    in_=sp[:].bitcast(BF16).rearrange("p (u r e) -> p r u e", u=2, e=2),
-                    func=ACT.Silu,
+        ys = {}
+        bias_f = const.tile([P, OUT_F], F32)
+        ident_f = const.tile([P, P], F32)
+        ident_b = const.tile([P, P], BF16)
+        sq_bias = []
+        coef = []
+
+        with tc.tile_pool(name="head", bufs=1) as head:
+            x_nat = head.tile([P, 4 * IN_F], BF16)
+            nc.sync.dma_start(
+                out=x_nat[:].rearrange("p (m i) -> p m i", m=4),
+                in_=xf.rearrange("(m p) i -> p m i", p=P),
+            )
+            bias_bc = head.tile([P, OUT_F], BF16)
+            nc.gpsimd.dma_start(out=bias_bc[:], in_=base_b.partition_broadcast(P))
+            for i in range(3):
+                load_chunk(i)
+
+            make_identity(nc, ident_b[:])
+            make_identity(nc, ident_f[:])
+            for e in range(2):
+                vals = head.tile([P, P], F32, name="vals%d" % e)
+                for q in range(4):
+                    nc.vector.memset(vals[:].rearrange("p (f s) -> p f s", s=4)[:, :, q], float(2 * q + e))
+                nc.vector.tensor_tensor(out=vals[:], in0=vals[:], in1=ident_f[:], op=ALU.mult)
+                j_e = const.tile([P, 1], F32, name="grid_index%d" % e)
+                nc.vector.reduce_sum(out=j_e[:], in_=vals[:], axis=AX.X)
+                b_e = const.tile([P, 1], F32, name="sq_bias%d" % e)
+                nc.vector.tensor_scalar(
+                    out=b_e[:], in0=j_e[:], scalar1=-CINV * STEP, scalar2=2.0 * CINV, op0=ALU.mult, op1=ALU.add
                 )
-                codes = keep.tile([P, RH], U32, align_bytes=64, name="sq_%d_%d" % (r, g))
-                plane = keep.tile([P, RH], U8, align_bytes=64, name="ss_%d_%d" % (r, g))
-                nc.vector.quantize_mx(out=codes[:].bitcast(FP8X4), scales=plane[:], in_=grp[:])
-                acts[(("b", g), r)] = (codes, plane)
+                sq_bias.append(b_e)
+            fold = const.tile([P, 32], BF16)
+            fold2 = const.tile([P, 32], BF16)
+            nc.vector.tensor_tensor(out=fold[:], in0=ident_b[:, 0:32], in1=ident_b[:, 32:64], op=ALU.add)
+            nc.vector.tensor_tensor(out=fold2[:], in0=ident_b[:, 64:96], in1=ident_b[:, 96:128], op=ALU.add)
+            nc.vector.tensor_tensor(out=fold[:], in0=fold[:], in1=fold2[:], op=ALU.add)
+            for e in range(2):
+                c_e = const.tile([P, P], BF16, name="coef%d" % e)
+                c_v = c_e[:].rearrange("p (f s) -> p f s", s=4)
+                nc.vector.memset(c_e[0:64, :], 49.0)
+                for q in range(4):
+                    j = 2 * q + e
+                    nc.vector.memset(c_v[64:96, :, q], float(196 - 56 * j))
+                    nc.vector.memset(c_v[96:128, :, q], float((14 - 4 * j) * (14 - 4 * j)))
+                nc.vector.tensor_tensor(
+                    out=c_v, in0=c_v, in1=fold[:].unsqueeze(2).to_broadcast([P, 32, 4]), op=ALU.mult
+                )
+                coef.append(c_e)
 
-        prepared = {}
-
-        def prep_set(r, h):
-            if PATH[(r, h)] == "sel":
-                xp = wk.tile([P, 512], BF16, tag="wk", name="xp")
-                for s in range(2):
+            xts = head.tile([P, 2048], BF16)
+            for bnk in range(2):
+                xp = wk.tile([P, 1024], BF16, tag="wk", name="xp")
+                for j4 in range(4):
                     for mm in range(2):
-                        c0 = IN_F * (2 * r + mm) + P * (2 * h + s)
+                        c0 = IN_F * mm + P * (4 * bnk + j4)
                         nc.tensor.transpose(
-                            out=xp[:, 256 * s + P * mm : 256 * s + P * mm + P],
+                            out=xp[:, 256 * j4 + P * mm : 256 * j4 + P * mm + P],
                             in_=x_nat[:, c0 : c0 + P],
                             identity=ident_b[:],
                         )
-                xt = xtp.tile([P, 512], BF16, tag="xt", name="xt")
-                nc.vector.tensor_copy(out=xt[:], in_=xp[:])
-                prepared[(r, h)] = xt
-                return
-            y = ypool.tile([P, 2048], BF16, tag="y", name="y")
-            yv = y[:].rearrange("p (m j s f) -> p m j s f", m=2, j=8, s=4)
-            xs = x_nat[:].rearrange("p (m j f) -> p m j f", m=4, j=32)[:, 2 * r : 2 * r + 2, 8 * h : 8 * h + 8, :]
-            nc.gpsimd.tensor_scalar(
-                out=yv[:, :, :, 2, :], in0=xs, scalar1=CLAMP, scalar2=-CLAMP, op0=ALU.min, op1=ALU.max
+                nc.scalar.copy(out=xts[:, 1024 * bnk : 1024 * bnk + 1024], in_=xp[:])
+            xts_w = xts[:].bitcast(F32)
+            for d in range(4):
+                nc.scalar.dma_start(
+                    out=scr.rearrange("q (jt d) w -> q jt d w", d=4)[:, :, d, :],
+                    in_=xts_w[32 * d : 32 * d + 32, :].rearrange("p (jt w) -> p jt w", w=P),
+                )
+
+            for h in range(4):
+                eng = nc.vector if h < 2 else nc.gpsimd
+                y = keep.tile([P, 2048], BF16, name="y%d" % h)
+                yv = y[:].rearrange("p (m j s f) -> p m j s f", m=2, j=8, s=4)
+                xs = x_nat[:].rearrange("p (m j f) -> p m j f", m=4, j=32)[:, 2:4, 8 * h : 8 * h + 8, :]
+                eng.tensor_scalar(
+                    out=yv[:, :, :, 2, :], in0=xs, scalar1=CLAMP, scalar2=-CLAMP, op0=ALU.min, op1=ALU.max
+                )
+                sqr = head.tile([P, 512], F32, name="sqr%d" % (h // 2))
+                sv = sqr[:].rearrange("p (m j f) -> p m j f", m=2, j=8)
+                eng.tensor_tensor(out=sv, in0=yv[:, :, :, 2, :], in1=yv[:, :, :, 2, :], op=ALU.mult)
+                eng.tensor_tensor(out=yv[:, :, :, 0, :], in0=yv[:, :, :, 2, :], in1=yv[:, :, :, 2, :], op=ALU.mult)
+                eng.tensor_tensor(out=yv[:, :, :, 1, :], in0=sv, in1=yv[:, :, :, 0, :], op=ALU.subtract)
+                eng.memset(yv[:, :, :, 3, :], 1.0)
+                ys[h] = y
+
+            x_words = x_nat[:].bitcast(F32)
+            for r in range(2):
+                for g in range(2):
+                    sp = wk.tile([P, 512], F32, tag="wk", name="sp")
+                    for u in range(2):
+                        for mm in range(2):
+                            c0 = 512 * (2 * r + mm) + 256 * g + P * u
+                            nc.tensor.transpose(
+                                out=sp[:, 256 * u + P * mm : 256 * u + P * mm + P],
+                                in_=x_words[:, c0 : c0 + P],
+                                identity=ident_f[:],
+                            )
+                    grp = bgrps.tile([P, 4 * RH], BF16, align_bytes=64, tag="bgrp", name="sgrp")
+                    nc.scalar.activation(
+                        out=grp[:].rearrange("p (r u e) -> p r u e", u=2, e=2),
+                        in_=sp[:].bitcast(BF16).rearrange("p (u r e) -> p r u e", u=2, e=2),
+                        func=ACT.Silu,
+                    )
+                    codes = keep.tile([P, RH], U32, align_bytes=64, name="sq_%d_%d" % (r, g))
+                    plane = keep.tile([P, RH], U8, align_bytes=64, name="ss_%d_%d" % (r, g))
+                    nc.vector.quantize_mx(out=codes[:].bitcast(FP8X4), scales=plane[:], in_=grp[:])
+                    acts[(("b", g), r)] = (codes, plane)
+            nc.vector.tensor_copy(out=bias_f[:], in_=bias_bc[:])
+            load_x4(0, nc.scalar)
+            load_x4(1, nc.sync)
+
+        late = ctx.enter_context(tc.tile_pool(name="late", bufs=1))
+        ostage = ctx.enter_context(tc.tile_pool(name="ostage", bufs=2))
+
+        units = [(("b", g), half, 0) for g in range(2) for half in range(2)]
+        units += [
+            (("s", 4 * h + a), half, 1 + 2 * h + half) for h in range(4) for half in range(2) for a in range(4)
+        ]
+        wgrp_of = {}
+        banks = {}
+        wts = {}
+
+        def w_col(j, n, u):
+            kk, half, ci = units[j]
+            if kk[0] == "b":
+                return 512 * (4 * half + n) + 256 * kk[1] + P * u
+            return 1024 * n + P * (kk[1] % 4) + 512 * u
+
+        def w_transposes(s, b):
+            j, q = 2 * s + b // 2, b % 2
+            words = chunk_words[units[j][2]]
+            wt = wk.tile([P, 512], F32, tag="wk", name="wt")
+            for nn in range(2):
+                for u in range(2):
+                    c0 = w_col(j, 2 * q + nn, u)
+                    nc.tensor.transpose(
+                        out=wt[:, 256 * nn + P * u : 256 * nn + P * u + P],
+                        in_=words[:, c0 : c0 + P],
+                        identity=ident_f[:],
+                    )
+            banks[(s, b)] = wt
+
+        def w_evict(s, b):
+            j, q = 2 * s + b // 2, b % 2
+            if q == 0:
+                wgrp_of[j] = wgrps.tile([P, 4 * HALF], BF16, align_bytes=64, tag="wgrp", name="wgrp")
+            dst = wgrp_of[j][:].bitcast(F32)[:, 512 * q : 512 * q + 512].rearrange("p (n o u) -> p n o u", n=2, u=2)
+            srcv = banks[(s, b)][:].rearrange("p (n u o) -> p n o u", n=2, u=2)
+            if act_evicts(s, b):
+                nc.scalar.copy(out=dst, in_=srcv)
+            else:
+                nc.vector.tensor_copy(out=dst, in_=srcv)
+
+        def w_quantise(j):
+            kk, half, ci = units[j]
+            nm = "%s%d_%d" % (kk[0], kk[1], half)
+            codes = keep.tile([P, HALF], U32, align_bytes=64, name="wq_" + nm)
+            plane = keep.tile([P, HALF], U8, align_bytes=64, name="ws_" + nm)
+            nc.vector.quantize_mx(out=codes[:].bitcast(FP8X4), scales=plane[:], in_=wgrp_of[j][:])
+            wts[(kk, half)] = (codes, plane)
+
+        grp_of = {}
+
+        def basis_square(c):
+            h, a = divmod(c, 4)
+            src = x4s[h][:].rearrange("p (u a r) -> p u a r", u=2, a=4)[:, :, a, :]
+            qq = qpool.tile([P, 4 * RH], F32, tag="qq", name="qq")
+            for e in range(2):
+                nc.scalar.activation(
+                    out=qq[:].rearrange("p (u e r) -> p u e r", u=2, e=2)[:, :, e, :],
+                    in_=src,
+                    func=ACT.Square,
+                    bias=sq_bias[e][:, 0:1],
+                    scale=CINV,
+                )
+            grp = bgrps.tile([P, 4 * RH], BF16, align_bytes=64, tag="bgrp", name="bgrp")
+            nc.scalar.activation(
+                out=grp[:].rearrange("p (r t) -> p r t", t=4),
+                in_=qq[:].rearrange("p (t r) -> p r t", t=4),
+                func=ACT.Exp,
+                scale=-1.0,
             )
-            sqr = ypool.tile([P, 512], F32, tag="sqr", name="sqr")
-            sv = sqr[:].rearrange("p (m j f) -> p m j f", m=2, j=8)
-            nc.gpsimd.tensor_tensor(out=sv, in0=yv[:, :, :, 2, :], in1=yv[:, :, :, 2, :], op=ALU.mult)
-            nc.gpsimd.tensor_tensor(out=yv[:, :, :, 0, :], in0=yv[:, :, :, 2, :], in1=yv[:, :, :, 2, :], op=ALU.mult)
-            nc.gpsimd.tensor_tensor(out=yv[:, :, :, 1, :], in0=sv, in1=yv[:, :, :, 0, :], op=ALU.subtract)
-            nc.gpsimd.memset(yv[:, :, :, 3, :], 1.0)
-            yt = ytp.tile([P, 2048], BF16, tag="yt", name="yt")
+            grp_of[(c, 0)] = grp
+
+        yts = {}
+
+        def y_transposes(h):
+            yt = late.tile([P, 2048], BF16, name="yt%d" % h)
             for jh in range(2):
                 yp = wk.tile([P, 1024], BF16, tag="wk", name="yp")
                 for j4 in range(4):
@@ -194,104 +279,55 @@ def tile_kanlinear_kernel(tc, x, base_w, base_b, spline_w, out):
                         c0 = 1024 * mm + P * (4 * jh + j4)
                         nc.tensor.transpose(
                             out=yp[:, 256 * j4 + P * mm : 256 * j4 + P * mm + P],
-                            in_=y[:, c0 : c0 + P],
+                            in_=ys[h][:, c0 : c0 + P],
                             identity=ident_b[:],
                         )
                 nc.vector.tensor_copy(out=yt[:, 1024 * jh : 1024 * jh + 1024], in_=yp[:])
-            prepared[(r, h)] = yt
+            yts[h] = yt
 
-        def basis(c, r):
+        def basis_exponent(c):
             h, a = divmod(c, 4)
-            src = prepared[(r, h)]
             grp = bgrps.tile([P, 4 * RH], BF16, align_bytes=64, tag="bgrp", name="bgrp")
-            if PATH[(r, h)] == "sel":
-                x4 = wk.tile([P, 512], F32, tag="wk", name="x4")
-                for u in range(2):
-                    nc.tensor.matmul(
-                        out=x4[:, RH * u : RH * u + RH],
-                        lhsT=sel[:, P * a : P * a + P],
-                        rhs=src[:, RH * u : RH * u + RH],
-                        start=True,
-                        stop=True,
-                    )
-                qq = qpool.tile([P, 4 * RH], F32, tag="qq", name="qq")
-                for e in range(2):
-                    nc.scalar.activation(
-                        out=qq[:].rearrange("p (u e r) -> p u e r", u=2, e=2)[:, :, e, :],
-                        in_=x4[:].rearrange("p (u r) -> p u r", u=2),
-                        func=ACT.Square,
-                        bias=sq_bias[e][:, 0:1],
-                        scale=CINV,
-                    )
-                nc.scalar.activation(
-                    out=grp[:].rearrange("p (r t) -> p r t", t=4),
-                    in_=qq[:].rearrange("p (t r) -> p r t", t=4),
-                    func=ACT.Exp,
-                    scale=-1.0,
-                )
-            else:
-                for mm in range(2):
-                    ex = wk.tile([P, 512], F32, tag="wk", name="ex")
-                    for u in range(2):
-                        for e in range(2):
-                            c0 = 256 * (a + 4 * u) + P * mm
-                            nc.tensor.matmul(
-                                out=ex[:, P * (2 * u + e) : P * (2 * u + e) + P],
-                                lhsT=coef[e][:],
-                                rhs=src[:, c0 : c0 + P],
-                                start=True,
-                                stop=True,
-                            )
-                    nc.scalar.activation(
-                        out=grp[:, 512 * mm : 512 * mm + 512].rearrange("p (r t) -> p r t", t=4),
-                        in_=ex[:].rearrange("p (t r) -> p r t", t=4),
-                        func=ACT.Exp,
-                        scale=-(CINV / 7.0) * (CINV / 7.0),
-                    )
-            acts[(("s", c), r)] = quantise(bc0 if r == 0 else bc1, grp, "%d_%d" % (c, r))
-
-        wts = {}
-        counter = [0]
-
-        def weights(kk, half, words, col_of):
-            wgrp = wgrps.tile([P, 4 * HALF], BF16, align_bytes=64, tag="wgrp", name="wgrp")
-            wgrp_w = wgrp[:].bitcast(F32)
-            for q in range(2):
-                wt = wk.tile([P, 512], F32, tag="wk", name="wt")
-                for nn in range(2):
-                    for u in range(2):
-                        c0 = col_of(2 * q + nn, u)
-                        nc.tensor.transpose(
-                            out=wt[:, 256 * nn + P * u : 256 * nn + P * u + P],
-                            in_=words[:, c0 : c0 + P],
-                            identity=ident_f[:],
-                        )
-                dst = wgrp_w[:, 512 * q : 512 * q + 512].rearrange("p (n o u) -> p n o u", n=2, u=2)
-                srcv = wt[:].rearrange("p (n u o) -> p n o u", n=2, u=2)
-                if q == 1 and counter[0] % 2 == 0:
-                    nc.scalar.copy(out=dst, in_=srcv)
-                else:
-                    nc.vector.tensor_copy(out=dst, in_=srcv)
-            counter[0] += 1
-            nm = "%s%d_%d" % (kk[0], kk[1], half)
-            codes = keep.tile([P, HALF], U32, align_bytes=64, name="wq_" + nm)
-            plane = keep.tile([P, HALF], U8, align_bytes=64, name="ws_" + nm)
-            nc.vector.quantize_mx(out=codes[:].bitcast(FP8X4), scales=plane[:], in_=wgrp[:])
-            wts[(kk, half)] = (codes, plane)
-
-        def mx(accs, kk, r, half):
-            a_c, a_p = acts[(kk, r)]
-            w_c, w_p = wts[(kk, half)]
             for mm in range(2):
-                nc.tensor.matmul_mx(
-                    out=accs[(mm, half)][:],
-                    lhsT=a_c[:, P * mm : P * mm + P].bitcast(FP8X4),
-                    lhsT_scale=a_p[:, P * mm : P * mm + P],
-                    rhs=w_c[:].bitcast(FP8X4),
-                    rhs_scale=w_p[:],
-                    start=(kk == ("b", 0)),
-                    stop=(kk == ("s", 15)),
+                ex = wk.tile([P, 512], F32, tag="wk", name="ex")
+                for u in range(2):
+                    for e in range(2):
+                        c0 = 256 * (a + 4 * u) + P * mm
+                        nc.tensor.matmul(
+                            out=ex[:, P * (2 * u + e) : P * (2 * u + e) + P],
+                            lhsT=coef[e][:],
+                            rhs=yts[h][:, c0 : c0 + P],
+                            start=True,
+                            stop=True,
+                        )
+                nc.scalar.activation(
+                    out=grp[:, 512 * mm : 512 * mm + 512].rearrange("p (r t) -> p r t", t=4),
+                    in_=ex[:].rearrange("p (t r) -> p r t", t=4),
+                    func=ACT.Exp,
+                    scale=-(CINV / 7.0) * (CINV / 7.0),
                 )
+            grp_of[(c, 1)] = grp
+
+        def basis_quantise(c, r):
+            codes = bcp.tile([P, RH], U32, align_bytes=64, tag="codes", name="bq")
+            plane = bcp.tile([P, RH], U8, align_bytes=64, tag="plane", name="bs")
+            nc.vector.quantize_mx(out=codes[:].bitcast(FP8X4), scales=plane[:], in_=grp_of[(c, r)][:])
+            acts[(("s", c), r)] = (codes, plane)
+
+        def mx(accs, kk, r):
+            a_c, a_p = acts[(kk, r)]
+            for half in range(2):
+                w_c, w_p = wts[(kk, half)]
+                for mm in range(2):
+                    nc.tensor.matmul_mx(
+                        out=accs[(mm, half)][:],
+                        lhsT=a_c[:, P * mm : P * mm + P].bitcast(FP8X4),
+                        lhsT_scale=a_p[:, P * mm : P * mm + P],
+                        rhs=w_c[:].bitcast(FP8X4),
+                        rhs_scale=w_p[:],
+                        start=(kk == ("b", 0)),
+                        stop=(kk == ("s", 15)),
+                    )
 
         def new_accs():
             accs = {}
@@ -300,48 +336,57 @@ def tile_kanlinear_kernel(tc, x, base_w, base_b, spline_w, out):
                     accs[(mm, half)] = accp.tile([P, HALF], F32, tag="acc", name="acc%d%d" % (mm, half))
             return accs
 
-        def finish(accs, r, half):
-            cols = slice(HALF * half, HALF * half + HALF)
-            for mm in range(2):
-                res = ostage.tile([P, HALF], F32, tag="res", name="res")
-                nc.vector.tensor_tensor(out=res[:], in0=accs[(mm, half)][:], in1=bias_f[:, cols], op=ALU.add)
-                r0 = RH * r + P * mm
-                nc.sync.dma_start(out=of[r0 : r0 + P, cols], in_=res[:])
+        def finish(accs, r):
+            for half in range(2):
+                cols = slice(HALF * half, HALF * half + HALF)
+                for mm in range(2):
+                    res = ostage.tile([P, HALF], F32, tag="res", name="res")
+                    nc.vector.tensor_tensor(out=res[:], in0=accs[(mm, half)][:], in1=bias_f[:, cols], op=ALU.add)
+                    r0 = RH * r + P * mm
+                    nc.sync.dma_start(out=of[r0 : r0 + P, cols], in_=res[:])
 
         accs = new_accs()
-        prep_set(0, 0)
-        for g in range(2):
-            for half in range(2):
-                weights(("b", g), half, chunk_words[0], lambda n, u: 512 * (4 * half + n) + 256 * g + P * u)
-                mx(accs, ("b", g), 0, half)
-        for h in range(4):
-            if h < 3:
-                prep_set(0, h + 1)
-                prep_set(1, h)
-            for half in range(2):
-                i = 1 + 2 * h + half
-                if i + 2 <= 8:
-                    chunk_words[i + 2] = load_chunk(i + 2)
-                for a in range(4):
-                    c = 4 * h + a
-                    if half == 0:
-                        basis(c, 0)
-                    weights(("s", c), half, chunk_words[i], lambda n, u: 1024 * n + P * a + 512 * u)
-                    mx(accs, ("s", c), 0, half)
-        for half in range(2):
-            finish(accs, 0, half)
+        for s in range(22):
+            if s < 18:
+                for b in range(4):
+                    w_transposes(s, b)
+                w_evict(s, 0)
+                w_evict(s, 1)
+                if s > 0:
+                    w_quantise(2 * s - 1)
+                w_evict(s, 2)
+                w_evict(s, 3)
+                w_quantise(2 * s)
+                if s % 2 == 1 and (s - 1) // 2 + 3 <= 8:
+                    load_chunk((s - 1) // 2 + 3)
+            if s == 18:
+                w_quantise(35)
+            if s in (18, 19):
+                y_transposes(2 * (s - 18))
+                y_transposes(2 * (s - 18) + 1)
+            if 0 <= s - 2 < 16:
+                basis_square(s - 2)
+            if s in (5, 9):
+                load_x4((s + 3) // 4, nc.sync)
+            if 0 <= s - 4 < 16:
+                basis_quantise(s - 4, 0)
+            if s in (2, 3):
+                mx(accs, ("b", s - 2), 0)
+            if 0 <= s - 6 < 16:
+                mx(accs, ("s", s - 6), 0)
+            if s >= 20:
+                basis_exponent(s - 20)
+            if s == 21:
+                basis_quantise(0, 1)
+        finish(accs, 0)
 
         accs = new_accs()
         for g in range(2):
-            for half in range(2):
-                mx(accs, ("b", g), 1, half)
-        for h in range(4):
-            for a in range(4):
-                c = 4 * h + a
-                basis(c, 1)
-                for half in range(2):
-                    mx(accs, ("s", c), 1, half)
-            if h == 0:
-                prep_set(1, 3)
-        for half in range(2):
-            finish(accs, 1, half)
+            mx(accs, ("b", g), 1)
+        for i in range(2, 18):
+            if i < 16:
+                basis_exponent(i)
+            if i - 1 < 16:
+                basis_quantise(i - 1, 1)
+            mx(accs, ("s", i - 2), 1)
+        finish(accs, 1)

@@ -26,10 +26,13 @@ CLAMP = 64.0
 FLOPS = 2 * ROWS * OUT_F * (IN_F + IN_F * GRID)
 
 
-def act_evicts(s, b):
-    if b == 3:
-        return s >= 1 and (s <= 3 or s % 3 != 0)
-    return b == 1 and s in (1, 2)
+N_UNITS = 36
+MX_LAG = 8
+BASIS_AT = 7
+
+
+def act_evicts(j, q):
+    return q == 1 and (j < 5 or j % 10 in (1, 4, 7))
 
 
 def tile_kanlinear_kernel(tc, x, base_w, base_b, spline_w, out):
@@ -37,7 +40,7 @@ def tile_kanlinear_kernel(tc, x, base_w, base_b, spline_w, out):
     xf = x.flatten_outer_dims()
     of = out.flatten_outer_dims()
     sw = spline_w.rearrange("o i g -> o (i g)")
-    scr = of[384:512, :].rearrange("(q a) (b w) -> q (a b) w", a=4, w=P)
+    scr = of[384:512, :]
 
     with ExitStack() as ctx:
         ctx.enter_context(tc.manual_schedule())
@@ -56,19 +59,11 @@ def tile_kanlinear_kernel(tc, x, base_w, base_b, spline_w, out):
 
         def load_chunk(i):
             ch = chunks.tile([P, 8192], BF16, tag="chunk", name="chunk%d" % i)
-            if i == 0:
-                for half in range(2):
-                    nc.sync.dma_start(
-                        out=ch[:, 4096 * half : 4096 * half + 4096].rearrange("p (n k) -> p n k", n=4),
-                        in_=base_w[HALF * half : HALF * half + HALF, :].rearrange("(n p) k -> p n k", p=P),
-                    )
-            else:
-                h, half = divmod(i - 1, 2)
+            src = base_w if i == 0 else sw[:, 1024 * (i - 1) : 1024 * i]
+            for half in range(2):
                 nc.sync.dma_start(
-                    out=ch[:].rearrange("p (n k) -> p n k", n=4),
-                    in_=sw[HALF * half : HALF * half + HALF, 2048 * h : 2048 * h + 2048].rearrange(
-                        "(n p) k -> p n k", p=P
-                    ),
+                    out=ch[:, 4096 * half : 4096 * half + 4096].rearrange("p (n k) -> p n k", n=4),
+                    in_=src[HALF * half : HALF * half + HALF, :].rearrange("(n p) k -> p n k", p=P),
                 )
             chunk_words[i] = ch[:].bitcast(F32)
 
@@ -79,7 +74,8 @@ def tile_kanlinear_kernel(tc, x, base_w, base_b, spline_w, out):
             tw = t[:].bitcast(F32)
             for s in range(4):
                 queue.dma_start(
-                    out=tw[s:P:4, :], in_=scr[:, 8 * h : 8 * h + 8, :].rearrange("q j w -> q (j w)")
+                    out=tw[s:P:4, :].rearrange("p (d w) -> p d w", d=4),
+                    in_=scr[:, 256 * h : 256 * h + 256].rearrange("(d q) w -> q d w", q=32),
                 )
             x4s[h] = t
 
@@ -146,11 +142,8 @@ def tile_kanlinear_kernel(tc, x, base_w, base_b, spline_w, out):
                             identity=ident_b[:],
                         )
                 nc.scalar.copy(out=xts[:, 1024 * bnk : 1024 * bnk + 1024], in_=xp[:])
-            xts_w = xts[:].bitcast(F32)
-            for d in range(4):
                 nc.scalar.dma_start(
-                    out=scr.rearrange("q (jt d) w -> q jt d w", d=4)[:, :, d, :],
-                    in_=xts_w[32 * d : 32 * d + 32, :].rearrange("p (jt w) -> p jt w", w=P),
+                    out=scr[:, 512 * bnk : 512 * bnk + 512], in_=xts[:].bitcast(F32)[:, 512 * bnk : 512 * bnk + 512]
                 )
 
             for h in range(4):
@@ -198,41 +191,31 @@ def tile_kanlinear_kernel(tc, x, base_w, base_b, spline_w, out):
         late = ctx.enter_context(tc.tile_pool(name="late", bufs=1))
         ostage = ctx.enter_context(tc.tile_pool(name="ostage", bufs=2))
 
-        units = [(("b", g), half, 0) for g in range(2) for half in range(2)]
-        units += [
-            (("s", 4 * h + a), half, 1 + 2 * h + half) for h in range(4) for half in range(2) for a in range(4)
-        ]
+        units = [(("b", g), half, 0) for half in range(2) for g in range(2)]
+        units += [(("s", c), half, 1 + c // 2) for c in range(16) for half in range(2)]
         wgrp_of = {}
         banks = {}
         wts = {}
 
-        def w_col(j, n, u):
+        def w_transposes(j, q):
             kk, half, ci = units[j]
-            if kk[0] == "b":
-                return 512 * (4 * half + n) + 256 * kk[1] + P * u
-            return 1024 * n + P * (kk[1] % 4) + 512 * u
-
-        def w_transposes(s, b):
-            j, q = 2 * s + b // 2, b % 2
-            words = chunk_words[units[j][2]]
             wt = wk.tile([P, 512], F32, tag="wk", name="wt")
             for nn in range(2):
                 for u in range(2):
-                    c0 = w_col(j, 2 * q + nn, u)
+                    c0 = 512 * (4 * half + 2 * q + nn) + 256 * (kk[1] % 2) + P * u
                     nc.tensor.transpose(
                         out=wt[:, 256 * nn + P * u : 256 * nn + P * u + P],
-                        in_=words[:, c0 : c0 + P],
+                        in_=chunk_words[ci][:, c0 : c0 + P],
                         identity=ident_f[:],
                     )
-            banks[(s, b)] = wt
+            banks[(j, q)] = wt
 
-        def w_evict(s, b):
-            j, q = 2 * s + b // 2, b % 2
+        def w_evict(j, q):
             if q == 0:
                 wgrp_of[j] = wgrps.tile([P, 4 * HALF], BF16, align_bytes=64, tag="wgrp", name="wgrp")
             dst = wgrp_of[j][:].bitcast(F32)[:, 512 * q : 512 * q + 512].rearrange("p (n o u) -> p n o u", n=2, u=2)
-            srcv = banks[(s, b)][:].rearrange("p (n u o) -> p n o u", n=2, u=2)
-            if act_evicts(s, b):
+            srcv = banks[(j, q)][:].rearrange("p (n u o) -> p n o u", n=2, u=2)
+            if act_evicts(j, q):
                 nc.scalar.copy(out=dst, in_=srcv)
             else:
                 nc.vector.tensor_copy(out=dst, in_=srcv)
@@ -247,9 +230,12 @@ def tile_kanlinear_kernel(tc, x, base_w, base_b, spline_w, out):
 
         grp_of = {}
 
-        def basis_square(c):
+        qq_of = {}
+
+        def basis_squares(c):
             h, a = divmod(c, 4)
-            src = x4s[h][:].rearrange("p (u a r) -> p u a r", u=2, a=4)[:, :, a, :]
+            d0 = 2 * (a % 2)
+            src = x4s[h][:].rearrange("p (d t r) -> p d t r", d=4, t=2)[:, d0 : d0 + 2, a // 2, :]
             qq = qpool.tile([P, 4 * RH], F32, tag="qq", name="qq")
             for e in range(2):
                 nc.scalar.activation(
@@ -259,10 +245,13 @@ def tile_kanlinear_kernel(tc, x, base_w, base_b, spline_w, out):
                     bias=sq_bias[e][:, 0:1],
                     scale=CINV,
                 )
+            qq_of[c] = qq
+
+        def basis_exp(c):
             grp = bgrps.tile([P, 4 * RH], BF16, align_bytes=64, tag="bgrp", name="bgrp")
             nc.scalar.activation(
                 out=grp[:].rearrange("p (r t) -> p r t", t=4),
-                in_=qq[:].rearrange("p (t r) -> p r t", t=4),
+                in_=qq_of[c][:].rearrange("p (t r) -> p r t", t=4),
                 func=ACT.Exp,
                 scale=-1.0,
             )
@@ -270,20 +259,19 @@ def tile_kanlinear_kernel(tc, x, base_w, base_b, spline_w, out):
 
         yts = {}
 
-        def y_transposes(h):
-            yt = late.tile([P, 2048], BF16, name="yt%d" % h)
-            for jh in range(2):
-                yp = wk.tile([P, 1024], BF16, tag="wk", name="yp")
-                for j4 in range(4):
-                    for mm in range(2):
-                        c0 = 1024 * mm + P * (4 * jh + j4)
-                        nc.tensor.transpose(
-                            out=yp[:, 256 * j4 + P * mm : 256 * j4 + P * mm + P],
-                            in_=ys[h][:, c0 : c0 + P],
-                            identity=ident_b[:],
-                        )
-                nc.vector.tensor_copy(out=yt[:, 1024 * jh : 1024 * jh + 1024], in_=yp[:])
-            yts[h] = yt
+        def y_transposes(h, jh):
+            if jh == 0:
+                yts[h] = late.tile([P, 2048], BF16, name="yt%d" % h)
+            yp = wk.tile([P, 1024], BF16, tag="wk", name="yp")
+            for j4 in range(4):
+                for mm in range(2):
+                    c0 = 1024 * mm + P * (4 * jh + j4)
+                    nc.tensor.transpose(
+                        out=yp[:, 256 * j4 + P * mm : 256 * j4 + P * mm + P],
+                        in_=ys[h][:, c0 : c0 + P],
+                        identity=ident_b[:],
+                    )
+            nc.vector.tensor_copy(out=yts[h][:, 1024 * jh : 1024 * jh + 1024], in_=yp[:])
 
         def basis_exponent(c):
             h, a = divmod(c, 4)
@@ -292,7 +280,7 @@ def tile_kanlinear_kernel(tc, x, base_w, base_b, spline_w, out):
                 ex = wk.tile([P, 512], F32, tag="wk", name="ex")
                 for u in range(2):
                     for e in range(2):
-                        c0 = 256 * (a + 4 * u) + P * mm
+                        c0 = 256 * (2 * a + u) + P * mm
                         nc.tensor.matmul(
                             out=ex[:, P * (2 * u + e) : P * (2 * u + e) + P],
                             lhsT=coef[e][:],
@@ -314,20 +302,20 @@ def tile_kanlinear_kernel(tc, x, base_w, base_b, spline_w, out):
             nc.vector.quantize_mx(out=codes[:].bitcast(FP8X4), scales=plane[:], in_=grp_of[(c, r)][:])
             acts[(("s", c), r)] = (codes, plane)
 
-        def mx(accs, kk, r):
+        def mx(accs, j, r):
+            kk, half, ci = units[j]
             a_c, a_p = acts[(kk, r)]
-            for half in range(2):
-                w_c, w_p = wts[(kk, half)]
-                for mm in range(2):
-                    nc.tensor.matmul_mx(
-                        out=accs[(mm, half)][:],
-                        lhsT=a_c[:, P * mm : P * mm + P].bitcast(FP8X4),
-                        lhsT_scale=a_p[:, P * mm : P * mm + P],
-                        rhs=w_c[:].bitcast(FP8X4),
-                        rhs_scale=w_p[:],
-                        start=(kk == ("b", 0)),
-                        stop=(kk == ("s", 15)),
-                    )
+            w_c, w_p = wts[(kk, half)]
+            for mm in range(2):
+                nc.tensor.matmul_mx(
+                    out=accs[(mm, half)][:],
+                    lhsT=a_c[:, P * mm : P * mm + P].bitcast(FP8X4),
+                    lhsT_scale=a_p[:, P * mm : P * mm + P],
+                    rhs=w_c[:].bitcast(FP8X4),
+                    rhs_scale=w_p[:],
+                    start=(kk == ("b", 0)),
+                    stop=(kk == ("s", 15)),
+                )
 
         def new_accs():
             accs = {}
@@ -346,47 +334,44 @@ def tile_kanlinear_kernel(tc, x, base_w, base_b, spline_w, out):
                     nc.sync.dma_start(out=of[r0 : r0 + P, cols], in_=res[:])
 
         accs = new_accs()
-        for s in range(22):
-            if s < 18:
-                for b in range(4):
-                    w_transposes(s, b)
-                w_evict(s, 0)
-                w_evict(s, 1)
-                if s > 0:
-                    w_quantise(2 * s - 1)
-                w_evict(s, 2)
-                w_evict(s, 3)
-                w_quantise(2 * s)
-                if s % 2 == 1 and (s - 1) // 2 + 3 <= 8:
-                    load_chunk((s - 1) // 2 + 3)
-            if s == 18:
-                w_quantise(35)
-            if s in (18, 19):
-                y_transposes(2 * (s - 18))
-                y_transposes(2 * (s - 18) + 1)
-            if 0 <= s - 2 < 16:
-                basis_square(s - 2)
-            if s in (5, 9):
-                load_x4((s + 3) // 4, nc.sync)
-            if 0 <= s - 4 < 16:
-                basis_quantise(s - 4, 0)
-            if s in (2, 3):
-                mx(accs, ("b", s - 2), 0)
-            if 0 <= s - 6 < 16:
-                mx(accs, ("s", s - 6), 0)
-            if s >= 20:
-                basis_exponent(s - 20)
-            if s == 21:
-                basis_quantise(0, 1)
+        for j in range(N_UNITS + MX_LAG):
+            if j < N_UNITS:
+                for q in range(2):
+                    w_transposes(j, q)
+                for q in range(2):
+                    w_evict(j, q)
+                if j % 4 == 3 and j // 4 + 3 <= 8:
+                    load_chunk(j // 4 + 3)
+            else:
+                y_transposes((j - N_UNITS) // 2, (j - N_UNITS) % 2)
+            if 1 <= j <= N_UNITS:
+                w_quantise(j - 1)
+            c, part = divmod(j - BASIS_AT, 2)
+            if 0 <= c < 16:
+                if part == 0:
+                    basis_squares(c)
+                    if c in (3, 7):
+                        load_x4(c // 4 + 2, nc.sync)
+                else:
+                    basis_exp(c)
+            c, part = divmod(j - BASIS_AT - 3, 2)
+            if 0 <= c < 16 and part == 0:
+                basis_quantise(c, 0)
+            if j >= MX_LAG:
+                mx(accs, j - MX_LAG, 0)
+        basis_exponent(0)
+        basis_exponent(1)
+        basis_quantise(0, 1)
         finish(accs, 0)
 
         accs = new_accs()
-        for g in range(2):
-            mx(accs, ("b", g), 1)
+        for j in range(4):
+            mx(accs, j, 1)
         for i in range(2, 18):
             if i < 16:
                 basis_exponent(i)
             if i - 1 < 16:
                 basis_quantise(i - 1, 1)
-            mx(accs, ("s", i - 2), 1)
+            mx(accs, 4 + 2 * (i - 2), 1)
+            mx(accs, 5 + 2 * (i - 2), 1)
         finish(accs, 1)

@@ -21,18 +21,21 @@ HALF = 512
 RH = 256
 STEP = 4.0 / 7.0
 CINV = 1.0 / (STEP + 1e-06)
-CLAMP = 64.0
 
 FLOPS = 2 * ROWS * OUT_F * (IN_F + IN_F * GRID)
 
-
 N_UNITS = 36
+HEAD_UNITS = 5
 MX_LAG = 8
 BASIS_AT = 7
 
 
 def act_evicts(j, q):
-    return q == 1 and (j < 5 or j % 10 in (1, 4, 7))
+    return q == 1 and (j < BASIS_AT or j % 10 not in (2, 5, 8))
+
+
+def vector_squares(c):
+    return c % 3 != 0
 
 
 def tile_kanlinear_kernel(tc, x, base_w, base_b, spline_w, out):
@@ -40,7 +43,7 @@ def tile_kanlinear_kernel(tc, x, base_w, base_b, spline_w, out):
     xf = x.flatten_outer_dims()
     of = out.flatten_outer_dims()
     sw = spline_w.rearrange("o i g -> o (i g)")
-    scr = of[384:512, :]
+    scr = [of[384:512, :], of[256:384, :]]
 
     with ExitStack() as ctx:
         ctx.enter_context(tc.manual_schedule())
@@ -48,10 +51,8 @@ def tile_kanlinear_kernel(tc, x, base_w, base_b, spline_w, out):
         keep = ctx.enter_context(tc.tile_pool(name="keep", bufs=1))
         chunks = ctx.enter_context(tc.tile_pool(name="chunks", bufs=3))
         wgrps = ctx.enter_context(tc.tile_pool(name="wgrps", bufs=3))
-        x4p = ctx.enter_context(tc.tile_pool(name="x4p", bufs=2))
-        qpool = ctx.enter_context(tc.tile_pool(name="qpool", bufs=2))
+        qpool = ctx.enter_context(tc.tile_pool(name="qpool", bufs=3))
         bgrps = ctx.enter_context(tc.tile_pool(name="bgrps", bufs=3))
-        bcp = ctx.enter_context(tc.tile_pool(name="bcp", bufs=7))
         accp = ctx.enter_context(tc.psum_pool(name="accp", bufs=4))
         wk = ctx.enter_context(tc.psum_pool(name="wk", bufs=4))
 
@@ -67,129 +68,79 @@ def tile_kanlinear_kernel(tc, x, base_w, base_b, spline_w, out):
                 )
             chunk_words[i] = ch[:].bitcast(F32)
 
-        x4s = {}
+        x4s = [keep.tile([P, 8192], BF16, name="x4_%d" % r) for r in range(2)]
 
-        def load_x4(h, queue):
-            t = x4p.tile([P, 2048], BF16, tag="x4", name="x4_%d" % h)
-            tw = t[:].bitcast(F32)
+        def load_x4(r, j0, j1):
+            w0, w1 = P * j0, P * j1
+            tw = x4s[r][:].bitcast(F32).rearrange("p (d w) -> p d w", d=4)
             for s in range(4):
-                queue.dma_start(
-                    out=tw[s:P:4, :].rearrange("p (d w) -> p d w", d=4),
-                    in_=scr[:, 256 * h : 256 * h + 256].rearrange("(d q) w -> q d w", q=32),
+                nc.sync.dma_start(
+                    out=tw[s:P:4, :, w0:w1],
+                    in_=scr[r][:, w0:w1].rearrange("(d q) w -> q d w", q=32),
                 )
-            x4s[h] = t
 
         acts = {}
-        ys = {}
-        bias_f = const.tile([P, OUT_F], F32)
         ident_f = const.tile([P, P], F32)
         ident_b = const.tile([P, P], BF16)
-        sq_bias = []
-        coef = []
+        bias_bc = const.tile([P, OUT_F], BF16)
+        make_identity(nc, ident_b[:])
+        make_identity(nc, ident_f[:])
+        vals = const.tile([P, P], F32)
+        for q in range(4):
+            nc.vector.memset(vals[:].rearrange("p (f s) -> p f s", s=4)[:, :, q], float(2 * q))
+        nc.vector.tensor_tensor(out=vals[:], in0=vals[:], in1=ident_f[:], op=ALU.mult)
+        index2 = const.tile([P, 1], F32)
+        nc.vector.reduce_sum(out=index2[:], in_=vals[:], axis=AX.X)
 
-        with tc.tile_pool(name="head", bufs=1) as head:
-            x_nat = head.tile([P, 4 * IN_F], BF16)
-            nc.sync.dma_start(
-                out=x_nat[:].rearrange("p (m i) -> p m i", m=4),
-                in_=xf.rearrange("(m p) i -> p m i", p=P),
-            )
-            bias_bc = head.tile([P, OUT_F], BF16)
-            nc.gpsimd.dma_start(out=bias_bc[:], in_=base_b.partition_broadcast(P))
-            for i in range(3):
-                load_chunk(i)
+        def per_partition(name, mul, add):
+            t = const.tile([P, 1], F32, name=name)
+            nc.vector.tensor_scalar(out=t[:], in0=index2[:], scalar1=mul, scalar2=add, op0=ALU.mult, op1=ALU.add)
+            return t
 
-            make_identity(nc, ident_b[:])
-            make_identity(nc, ident_f[:])
-            for e in range(2):
-                vals = head.tile([P, P], F32, name="vals%d" % e)
-                for q in range(4):
-                    nc.vector.memset(vals[:].rearrange("p (f s) -> p f s", s=4)[:, :, q], float(2 * q + e))
-                nc.vector.tensor_tensor(out=vals[:], in0=vals[:], in1=ident_f[:], op=ALU.mult)
-                j_e = const.tile([P, 1], F32, name="grid_index%d" % e)
-                nc.vector.reduce_sum(out=j_e[:], in_=vals[:], axis=AX.X)
-                b_e = const.tile([P, 1], F32, name="sq_bias%d" % e)
-                nc.vector.tensor_scalar(
-                    out=b_e[:], in0=j_e[:], scalar1=-CINV * STEP, scalar2=2.0 * CINV, op0=ALU.mult, op1=ALU.add
-                )
-                sq_bias.append(b_e)
-            fold = const.tile([P, 32], BF16)
-            fold2 = const.tile([P, 32], BF16)
-            nc.vector.tensor_tensor(out=fold[:], in0=ident_b[:, 0:32], in1=ident_b[:, 32:64], op=ALU.add)
-            nc.vector.tensor_tensor(out=fold2[:], in0=ident_b[:, 64:96], in1=ident_b[:, 96:128], op=ALU.add)
-            nc.vector.tensor_tensor(out=fold[:], in0=fold[:], in1=fold2[:], op=ALU.add)
-            for e in range(2):
-                c_e = const.tile([P, P], BF16, name="coef%d" % e)
-                c_v = c_e[:].rearrange("p (f s) -> p f s", s=4)
-                nc.vector.memset(c_e[0:64, :], 49.0)
-                for q in range(4):
-                    j = 2 * q + e
-                    nc.vector.memset(c_v[64:96, :, q], float(196 - 56 * j))
-                    nc.vector.memset(c_v[96:128, :, q], float((14 - 4 * j) * (14 - 4 * j)))
-                nc.vector.tensor_tensor(
-                    out=c_v, in0=c_v, in1=fold[:].unsqueeze(2).to_broadcast([P, 32, 4]), op=ALU.mult
-                )
-                coef.append(c_e)
+        sq_bias = [per_partition("sq_bias%d" % e, -CINV * STEP, CINV * (2.0 - STEP * e)) for e in range(2)]
+        neg_mid = per_partition("neg_mid", -STEP, 2.0 - STEP / 2)
+        neg_mid_e = [per_partition("neg_mid%d" % e, -STEP, 2.0 - STEP / 2 + (STEP, -STEP)[e]) for e in range(2)]
+        exp_bias = per_partition("exp_bias", 0.0, -CINV * CINV * STEP * STEP / 4)
 
-            xts = head.tile([P, 2048], BF16)
+        def x_to_scratch(r):
             for bnk in range(2):
                 xp = wk.tile([P, 1024], BF16, tag="wk", name="xp")
                 for j4 in range(4):
                     for mm in range(2):
-                        c0 = IN_F * mm + P * (4 * bnk + j4)
+                        c0 = IN_F * (2 * r + mm) + P * (4 * bnk + j4)
                         nc.tensor.transpose(
                             out=xp[:, 256 * j4 + P * mm : 256 * j4 + P * mm + P],
                             in_=x_nat[:, c0 : c0 + P],
                             identity=ident_b[:],
                         )
-                nc.scalar.copy(out=xts[:, 1024 * bnk : 1024 * bnk + 1024], in_=xp[:])
+                nc.scalar.copy(out=xts[r][:, 1024 * bnk : 1024 * bnk + 1024], in_=xp[:])
                 nc.scalar.dma_start(
-                    out=scr[:, 512 * bnk : 512 * bnk + 512], in_=xts[:].bitcast(F32)[:, 512 * bnk : 512 * bnk + 512]
+                    out=scr[r][:, 512 * bnk : 512 * bnk + 512],
+                    in_=xts[r][:].bitcast(F32)[:, 512 * bnk : 512 * bnk + 512],
                 )
 
-            for h in range(4):
-                eng = nc.vector if h < 2 else nc.gpsimd
-                y = keep.tile([P, 2048], BF16, name="y%d" % h)
-                yv = y[:].rearrange("p (m j s f) -> p m j s f", m=2, j=8, s=4)
-                xs = x_nat[:].rearrange("p (m j f) -> p m j f", m=4, j=32)[:, 2:4, 8 * h : 8 * h + 8, :]
-                eng.tensor_scalar(
-                    out=yv[:, :, :, 2, :], in0=xs, scalar1=CLAMP, scalar2=-CLAMP, op0=ALU.min, op1=ALU.max
-                )
-                sqr = head.tile([P, 512], F32, name="sqr%d" % (h // 2))
-                sv = sqr[:].rearrange("p (m j f) -> p m j f", m=2, j=8)
-                eng.tensor_tensor(out=sv, in0=yv[:, :, :, 2, :], in1=yv[:, :, :, 2, :], op=ALU.mult)
-                eng.tensor_tensor(out=yv[:, :, :, 0, :], in0=yv[:, :, :, 2, :], in1=yv[:, :, :, 2, :], op=ALU.mult)
-                eng.tensor_tensor(out=yv[:, :, :, 1, :], in0=sv, in1=yv[:, :, :, 0, :], op=ALU.subtract)
-                eng.memset(yv[:, :, :, 3, :], 1.0)
-                ys[h] = y
-
+        def silu(r):
             x_words = x_nat[:].bitcast(F32)
-            for r in range(2):
-                for g in range(2):
-                    sp = wk.tile([P, 512], F32, tag="wk", name="sp")
-                    for u in range(2):
-                        for mm in range(2):
-                            c0 = 512 * (2 * r + mm) + 256 * g + P * u
-                            nc.tensor.transpose(
-                                out=sp[:, 256 * u + P * mm : 256 * u + P * mm + P],
-                                in_=x_words[:, c0 : c0 + P],
-                                identity=ident_f[:],
-                            )
-                    grp = bgrps.tile([P, 4 * RH], BF16, align_bytes=64, tag="bgrp", name="sgrp")
-                    nc.scalar.activation(
-                        out=grp[:].rearrange("p (r u e) -> p r u e", u=2, e=2),
-                        in_=sp[:].bitcast(BF16).rearrange("p (u r e) -> p r u e", u=2, e=2),
-                        func=ACT.Silu,
-                    )
-                    codes = keep.tile([P, RH], U32, align_bytes=64, name="sq_%d_%d" % (r, g))
-                    plane = keep.tile([P, RH], U8, align_bytes=64, name="ss_%d_%d" % (r, g))
-                    nc.vector.quantize_mx(out=codes[:].bitcast(FP8X4), scales=plane[:], in_=grp[:])
-                    acts[(("b", g), r)] = (codes, plane)
-            nc.vector.tensor_copy(out=bias_f[:], in_=bias_bc[:])
-            load_x4(0, nc.scalar)
-            load_x4(1, nc.sync)
-
-        late = ctx.enter_context(tc.tile_pool(name="late", bufs=1))
-        ostage = ctx.enter_context(tc.tile_pool(name="ostage", bufs=2))
+            for g in range(2):
+                sp = wk.tile([P, 512], F32, tag="wk", name="sp")
+                for u in range(2):
+                    for mm in range(2):
+                        c0 = 512 * (2 * r + mm) + 256 * g + P * u
+                        nc.tensor.transpose(
+                            out=sp[:, 256 * u + P * mm : 256 * u + P * mm + P],
+                            in_=x_words[:, c0 : c0 + P],
+                            identity=ident_f[:],
+                        )
+                grp = bgrps.tile([P, 4 * RH], BF16, align_bytes=64, tag="bgrp", name="sgrp")
+                nc.scalar.activation(
+                    out=grp[:].rearrange("p (r u e) -> p r u e", u=2, e=2),
+                    in_=sp[:].bitcast(BF16).rearrange("p (u r e) -> p r u e", u=2, e=2),
+                    func=ACT.Silu,
+                )
+                codes = keep.tile([P, RH], U32, align_bytes=64, name="sq_%d_%d" % (r, g))
+                plane = keep.tile([P, RH], U8, align_bytes=64, name="ss_%d_%d" % (r, g))
+                nc.vector.quantize_mx(out=codes[:].bitcast(FP8X4), scales=plane[:], in_=grp[:])
+                acts[(("b", g), r)] = (codes, plane)
 
         units = [(("b", g), half, 0) for half in range(2) for g in range(2)]
         units += [(("s", c), half, 1 + c // 2) for c in range(16) for half in range(2)]
@@ -229,72 +180,37 @@ def tile_kanlinear_kernel(tc, x, base_w, base_b, spline_w, out):
             wts[(kk, half)] = (codes, plane)
 
         grp_of = {}
-
         qq_of = {}
 
-        def basis_squares(c):
-            h, a = divmod(c, 4)
-            d0 = 2 * (a % 2)
-            src = x4s[h][:].rearrange("p (d t r) -> p d t r", d=4, t=2)[:, d0 : d0 + 2, a // 2, :]
+        def basis_squares(c, r, on_vector):
+            src = x4s[r][:].rearrange("p (d t r) -> p d t r", d=4, t=8)[:, 2 * (c % 2) : 2 * (c % 2) + 2, c // 2, :]
             qq = qpool.tile([P, 4 * RH], F32, tag="qq", name="qq")
-            for e in range(2):
-                nc.scalar.activation(
-                    out=qq[:].rearrange("p (u e r) -> p u e r", u=2, e=2)[:, :, e, :],
-                    in_=src,
-                    func=ACT.Square,
-                    bias=sq_bias[e][:, 0:1],
-                    scale=CINV,
-                )
-            qq_of[c] = qq
-
-        def basis_exp(c):
-            grp = bgrps.tile([P, 4 * RH], BF16, align_bytes=64, tag="bgrp", name="bgrp")
-            nc.scalar.activation(
-                out=grp[:].rearrange("p (r t) -> p r t", t=4),
-                in_=qq_of[c][:].rearrange("p (t r) -> p r t", t=4),
-                func=ACT.Exp,
-                scale=-1.0,
-            )
-            grp_of[(c, 0)] = grp
-
-        yts = {}
-
-        def y_transposes(h, jh):
-            if jh == 0:
-                yts[h] = late.tile([P, 2048], BF16, name="yt%d" % h)
-            yp = wk.tile([P, 1024], BF16, tag="wk", name="yp")
-            for j4 in range(4):
-                for mm in range(2):
-                    c0 = 1024 * mm + P * (4 * jh + j4)
-                    nc.tensor.transpose(
-                        out=yp[:, 256 * j4 + P * mm : 256 * j4 + P * mm + P],
-                        in_=ys[h][:, c0 : c0 + P],
-                        identity=ident_b[:],
+            qv = qq[:].rearrange("p (u e r) -> p u e r", u=2, e=2)
+            if on_vector:
+                mid = qpool.tile([P, 2 * RH], F32, tag="mid", name="mid")
+                mv = mid[:].rearrange("p (u r) -> p u r", u=2)
+                nc.vector.tensor_scalar(out=mv, in0=src, scalar1=neg_mid[:, 0:1], scalar2=None, op0=ALU.add)
+                for e in range(2):
+                    nc.vector.scalar_tensor_tensor(
+                        out=qv[:, :, e, :], in0=src, scalar=neg_mid_e[e][:, 0:1], in1=mv, op0=ALU.add, op1=ALU.mult
                     )
-            nc.vector.tensor_copy(out=yts[h][:, 1024 * jh : 1024 * jh + 1024], in_=yp[:])
+            else:
+                for e in range(2):
+                    nc.scalar.activation(
+                        out=qv[:, :, e, :], in_=src, func=ACT.Square, bias=sq_bias[e][:, 0:1], scale=CINV
+                    )
+            qq_of[(c, r)] = (qq, on_vector)
 
-        def basis_exponent(c):
-            h, a = divmod(c, 4)
+        def basis_exp(c, r):
+            qq, on_vector = qq_of[(c, r)]
             grp = bgrps.tile([P, 4 * RH], BF16, align_bytes=64, tag="bgrp", name="bgrp")
-            for mm in range(2):
-                ex = wk.tile([P, 512], F32, tag="wk", name="ex")
-                for u in range(2):
-                    for e in range(2):
-                        c0 = 256 * (2 * a + u) + P * mm
-                        nc.tensor.matmul(
-                            out=ex[:, P * (2 * u + e) : P * (2 * u + e) + P],
-                            lhsT=coef[e][:],
-                            rhs=yts[h][:, c0 : c0 + P],
-                            start=True,
-                            stop=True,
-                        )
-                nc.scalar.activation(
-                    out=grp[:, 512 * mm : 512 * mm + 512].rearrange("p (r t) -> p r t", t=4),
-                    in_=ex[:].rearrange("p (t r) -> p r t", t=4),
-                    func=ACT.Exp,
-                    scale=-(CINV / 7.0) * (CINV / 7.0),
-                )
-            grp_of[(c, 1)] = grp
+            dst = grp[:].rearrange("p (r t) -> p r t", t=4)
+            srcv = qq[:].rearrange("p (t r) -> p r t", t=4)
+            if on_vector:
+                nc.scalar.activation(out=dst, in_=srcv, func=ACT.Exp, bias=exp_bias[:, 0:1], scale=-CINV * CINV)
+            else:
+                nc.scalar.activation(out=dst, in_=srcv, func=ACT.Exp, scale=-1.0)
+            grp_of[(c, r)] = grp
 
         def basis_quantise(c, r):
             codes = bcp.tile([P, RH], U32, align_bytes=64, tag="codes", name="bq")
@@ -302,76 +218,120 @@ def tile_kanlinear_kernel(tc, x, base_w, base_b, spline_w, out):
             nc.vector.quantize_mx(out=codes[:].bitcast(FP8X4), scales=plane[:], in_=grp_of[(c, r)][:])
             acts[(("s", c), r)] = (codes, plane)
 
-        def mx(accs, j, r):
-            kk, half, ci = units[j]
+        def mx_one(accs, kk, half, mm, r):
             a_c, a_p = acts[(kk, r)]
             w_c, w_p = wts[(kk, half)]
-            for mm in range(2):
-                nc.tensor.matmul_mx(
-                    out=accs[(mm, half)][:],
-                    lhsT=a_c[:, P * mm : P * mm + P].bitcast(FP8X4),
-                    lhsT_scale=a_p[:, P * mm : P * mm + P],
-                    rhs=w_c[:].bitcast(FP8X4),
-                    rhs_scale=w_p[:],
-                    start=(kk == ("b", 0)),
-                    stop=(kk == ("s", 15)),
-                )
+            nc.tensor.matmul_mx(
+                out=accs[(mm, half)][:],
+                lhsT=a_c[:, P * mm : P * mm + P].bitcast(FP8X4),
+                lhsT_scale=a_p[:, P * mm : P * mm + P],
+                rhs=w_c[:].bitcast(FP8X4),
+                rhs_scale=w_p[:],
+                start=(kk == ("b", 0)),
+                stop=(kk == ("s", 15)),
+            )
 
-        def new_accs():
+        def mx(accs, j, r):
+            kk, half, ci = units[j]
+            for mm in range(2):
+                mx_one(accs, kk, half, mm, r)
+
+        def new_accs(pool, tag):
             accs = {}
             for half in range(2):
                 for mm in range(2):
-                    accs[(mm, half)] = accp.tile([P, HALF], F32, tag="acc", name="acc%d%d" % (mm, half))
+                    accs[(mm, half)] = pool.tile([P, HALF], F32, tag=tag, name="acc%d%d" % (mm, half))
             return accs
 
-        def finish(accs, r):
-            for half in range(2):
-                cols = slice(HALF * half, HALF * half + HALF)
-                for mm in range(2):
-                    res = ostage.tile([P, HALF], F32, tag="res", name="res")
-                    nc.vector.tensor_tensor(out=res[:], in0=accs[(mm, half)][:], in1=bias_f[:, cols], op=ALU.add)
-                    r0 = RH * r + P * mm
-                    nc.sync.dma_start(out=of[r0 : r0 + P, cols], in_=res[:])
+        def finish(accs, r, half, mm):
+            cols = slice(HALF * half, HALF * half + HALF)
+            res = ostage.tile([P, HALF], F32, tag="res", name="res")
+            nc.vector.tensor_tensor(out=res[:], in0=accs[(mm, half)][:], in1=bias_bc[:, cols], op=ALU.add)
+            r0 = RH * r + P * mm
+            nc.sync.dma_start(out=of[r0 : r0 + P, cols], in_=res[:])
 
-        accs = new_accs()
-        for j in range(N_UNITS + MX_LAG):
-            if j < N_UNITS:
-                for q in range(2):
-                    w_transposes(j, q)
-                for q in range(2):
-                    w_evict(j, q)
-                if j % 4 == 3 and j // 4 + 3 <= 8:
-                    load_chunk(j // 4 + 3)
-            else:
-                y_transposes((j - N_UNITS) // 2, (j - N_UNITS) % 2)
-            if 1 <= j <= N_UNITS:
+        accs = new_accs(accp, "acc")
+
+        def unit_step(j):
+            for q in range(2):
+                w_transposes(j, q)
+            for q in range(2):
+                w_evict(j, q)
+            if j % 4 == 3 and j // 4 + 3 <= 8:
+                load_chunk(j // 4 + 3)
+            if j == 24:
+                nc.sync.dma_start(out=bias_bc[:], in_=base_b.partition_broadcast(P))
+                load_x4(1, 0, 2)
+                load_x4(1, 2, 8)
+            if j == 2:
+                x_to_scratch(1)
+            if j == 4:
+                silu(1)
+            if j >= 1:
                 w_quantise(j - 1)
             c, part = divmod(j - BASIS_AT, 2)
-            if 0 <= c < 16:
+            if c >= 0:
                 if part == 0:
-                    basis_squares(c)
-                    if c in (3, 7):
-                        load_x4(c // 4 + 2, nc.sync)
+                    basis_squares(c, 0, False)
                 else:
-                    basis_exp(c)
+                    basis_exp(c, 0)
             c, part = divmod(j - BASIS_AT - 3, 2)
-            if 0 <= c < 16 and part == 0:
+            if c >= 0 and part == 0:
                 basis_quantise(c, 0)
             if j >= MX_LAG:
                 mx(accs, j - MX_LAG, 0)
-        basis_exponent(0)
-        basis_exponent(1)
-        basis_quantise(0, 1)
-        finish(accs, 0)
+        with tc.tile_pool(name="head", bufs=1) as head:
+            x_nat = head.tile([P, 4 * IN_F], BF16)
+            xts = [head.tile([P, 2048], BF16, name="xts%d" % r) for r in range(2)]
+            for r in range(2):
+                nc.sync.dma_start(
+                    out=x_nat[:, 2048 * r : 2048 * r + 2048].rearrange("p (m i) -> p m i", m=2),
+                    in_=xf[RH * r : RH * r + RH, :].rearrange("(m p) i -> p m i", p=P),
+                )
+            for i in range(2):
+                load_chunk(i)
+            x_to_scratch(0)
+            load_x4(0, 0, 2)
+            load_x4(0, 2, 8)
+            load_chunk(2)
+            silu(0)
+            for j in range(HEAD_UNITS):
+                unit_step(j)
+        bcp = ctx.enter_context(tc.tile_pool(name="bcp", bufs=8))
+        ostage = ctx.enter_context(tc.tile_pool(name="ostage", bufs=4))
+        for j in range(HEAD_UNITS, N_UNITS):
+            unit_step(j)
 
-        accs = new_accs()
+        w_quantise(N_UNITS - 1)
+        basis_exp(14, 0)
+        basis_quantise(13, 0)
+        basis_squares(15, 0, True)
+        basis_squares(0, 1, True)
+        basis_exp(15, 0)
+        basis_quantise(14, 0)
+        basis_squares(1, 1, True)
+        basis_exp(0, 1)
+        basis_quantise(15, 0)
+        for j in range(N_UNITS - MX_LAG, N_UNITS):
+            mx(accs, j, 0)
+        accs2 = new_accs(wk, "wk")
         for j in range(4):
-            mx(accs, j, 1)
-        for i in range(2, 18):
+            mx(accs2, j, 1)
+
+        for i in range(1, 17):
             if i < 16:
-                basis_exponent(i)
-            if i - 1 < 16:
-                basis_quantise(i - 1, 1)
-            mx(accs, 4 + 2 * (i - 2), 1)
-            mx(accs, 5 + 2 * (i - 2), 1)
-        finish(accs, 1)
+                if i + 1 < 16:
+                    basis_squares(i + 1, 1, vector_squares(i + 1))
+                basis_exp(i, 1)
+            basis_quantise(i - 1, 1)
+            if 3 <= i < 7:
+                finish(accs, 0, (i - 3) // 2, (i - 3) % 2)
+            if i <= 14:
+                for half in range(2):
+                    for mm in range(2):
+                        mx_one(accs2, ("s", i - 1), half, mm, 1)
+        for half in range(2):
+            for mm in range(2):
+                for c in (14, 15):
+                    mx_one(accs2, ("s", c), half, mm, 1)
+                finish(accs2, 1, half, mm)

@@ -204,8 +204,8 @@ def tile_kanlinear_kernel(tc, x, base_w, base_b, spline_w, out):
         def basis_exp(c, r):
             qq, on_vector = qq_of[(c, r)]
             grp = bgrps.tile([P, 4 * RH], BF16, align_bytes=64, tag="bgrp", name="bgrp")
-            dst = grp[:].rearrange("p (r t) -> p r t", t=4)
-            srcv = qq[:].rearrange("p (t r) -> p r t", t=4)
+            dst = grp[:].rearrange("p (c i t) -> p c t i", i=4, t=4)
+            srcv = qq[:].rearrange("p (t c i) -> p c t i", i=4, t=4)
             if on_vector:
                 nc.scalar.activation(out=dst, in_=srcv, func=ACT.Exp, bias=exp_bias[:, 0:1], scale=-CINV * CINV)
             else:

@@ -24,14 +24,14 @@ CINV = 1.0 / (STEP + 1e-06)
 
 FLOPS = 2 * ROWS * OUT_F * (IN_F + IN_F * GRID)
 
-N_UNITS = 36
-HEAD_UNITS = 5
-MX_LAG = 8
-BASIS_AT = 7
+N_STEPS = 18
+HEAD_STEPS = 3
+MX_LAG = 4
+BASIS_AT = 3
 
 
-def act_evicts(j, q):
-    return q == 1 and (j < BASIS_AT or j % 10 not in (2, 5, 8))
+def act_evicts(s, b):
+    return b == 1 or (b == 3 and (s < BASIS_AT or s % 3 == 0))
 
 
 def vector_squares(c):
@@ -50,7 +50,7 @@ def tile_kanlinear_kernel(tc, x, base_w, base_b, spline_w, out):
         const = ctx.enter_context(tc.tile_pool(name="const", bufs=1))
         keep = ctx.enter_context(tc.tile_pool(name="keep", bufs=1))
         chunks = ctx.enter_context(tc.tile_pool(name="chunks", bufs=3))
-        wgrps = ctx.enter_context(tc.tile_pool(name="wgrps", bufs=3))
+        wgrps = ctx.enter_context(tc.tile_pool(name="wgrps", bufs=4))
         qpool = ctx.enter_context(tc.tile_pool(name="qpool", bufs=3))
         bgrps = ctx.enter_context(tc.tile_pool(name="bgrps", bufs=3))
         accp = ctx.enter_context(tc.psum_pool(name="accp", bufs=4))
@@ -166,7 +166,7 @@ def tile_kanlinear_kernel(tc, x, base_w, base_b, spline_w, out):
                 wgrp_of[j] = wgrps.tile([P, 4 * HALF], BF16, align_bytes=64, tag="wgrp", name="wgrp")
             dst = wgrp_of[j][:].bitcast(F32)[:, 512 * q : 512 * q + 512].rearrange("p (n o u) -> p n o u", n=2, u=2)
             srcv = banks[(j, q)][:].rearrange("p (n u o) -> p n o u", n=2, u=2)
-            if act_evicts(j, q):
+            if act_evicts(j // 2, 2 * (j % 2) + q):
                 nc.scalar.copy(out=dst, in_=srcv)
             else:
                 nc.vector.tensor_copy(out=dst, in_=srcv)
@@ -252,34 +252,39 @@ def tile_kanlinear_kernel(tc, x, base_w, base_b, spline_w, out):
 
         accs = new_accs(accp, "acc")
 
-        def unit_step(j):
-            for q in range(2):
-                w_transposes(j, q)
-            for q in range(2):
-                w_evict(j, q)
-            if j % 4 == 3 and j // 4 + 3 <= 8:
-                load_chunk(j // 4 + 3)
-            if j == 24:
+        def step(s):
+            pair = (2 * s, 2 * s + 1)
+            for j in pair:
+                for q in range(2):
+                    w_transposes(j, q)
+            if s >= MX_LAG:
+                for j in pair:
+                    mx(accs, j - 2 * MX_LAG, 0)
+            w_evict(pair[0], 0)
+            w_evict(pair[0], 1)
+            c = s - BASIS_AT
+            if c >= 0:
+                basis_squares(c, 0, False)
+            w_evict(pair[1], 0)
+            w_evict(pair[1], 1)
+            if c >= 1:
+                basis_exp(c - 1, 0)
+            if s % 2 == 1 and s // 2 + 3 <= 8:
+                load_chunk(s // 2 + 3)
+            if s == 12:
                 nc.sync.dma_start(out=bias_bc[:], in_=base_b.partition_broadcast(P))
                 load_x4(1, 0, 2)
                 load_x4(1, 2, 8)
-            if j == 2:
+            if s == 1:
                 x_to_scratch(1)
-            if j == 4:
+            if s == 2:
                 silu(1)
-            if j >= 1:
-                w_quantise(j - 1)
-            c, part = divmod(j - BASIS_AT, 2)
-            if c >= 0:
-                if part == 0:
-                    basis_squares(c, 0, False)
-                else:
-                    basis_exp(c, 0)
-            c, part = divmod(j - BASIS_AT - 3, 2)
-            if c >= 0 and part == 0:
-                basis_quantise(c, 0)
-            if j >= MX_LAG:
-                mx(accs, j - MX_LAG, 0)
+            if s >= 1:
+                w_quantise(2 * s - 2)
+                w_quantise(2 * s - 1)
+            if c >= 2:
+                basis_quantise(c - 2, 0)
+
         with tc.tile_pool(name="head", bufs=1) as head:
             x_nat = head.tile([P, 4 * IN_F], BF16)
             xts = [head.tile([P, 2048], BF16, name="xts%d" % r) for r in range(2)]
@@ -295,14 +300,15 @@ def tile_kanlinear_kernel(tc, x, base_w, base_b, spline_w, out):
             load_x4(0, 2, 8)
             load_chunk(2)
             silu(0)
-            for j in range(HEAD_UNITS):
-                unit_step(j)
+            for s in range(HEAD_STEPS):
+                step(s)
         bcp = ctx.enter_context(tc.tile_pool(name="bcp", bufs=8))
         ostage = ctx.enter_context(tc.tile_pool(name="ostage", bufs=4))
-        for j in range(HEAD_UNITS, N_UNITS):
-            unit_step(j)
+        for s in range(HEAD_STEPS, N_STEPS):
+            step(s)
 
-        w_quantise(N_UNITS - 1)
+        w_quantise(2 * N_STEPS - 2)
+        w_quantise(2 * N_STEPS - 1)
         basis_exp(14, 0)
         basis_quantise(13, 0)
         basis_squares(15, 0, True)
@@ -312,7 +318,7 @@ def tile_kanlinear_kernel(tc, x, base_w, base_b, spline_w, out):
         basis_squares(1, 1, True)
         basis_exp(0, 1)
         basis_quantise(15, 0)
-        for j in range(N_UNITS - MX_LAG, N_UNITS):
+        for j in range(2 * (N_STEPS - MX_LAG), 2 * N_STEPS):
             mx(accs, j, 0)
         accs2 = new_accs(wk, "wk")
         for j in range(4):

@@ -25,17 +25,18 @@ CINV = 1.0 / (STEP + 1e-06)
 FLOPS = 2 * ROWS * OUT_F * (IN_F + IN_F * GRID)
 
 N_STEPS = 18
-HEAD_STEPS = 3
-MX_LAG = 4
-BASIS_AT = 3
+HEAD_STEPS = 8
+MX_LAG = 2
+N_CHUNKS = 6
+N_DIRECT = 4
 
 
 def act_evicts(s, b):
-    return b == 1 or (b == 3 and (s < BASIS_AT or s % 3 == 0))
+    return s >= 2 and (b == 1 or (b == 3 and s % 3 == 2))
 
 
-def vector_squares(c):
-    return c % 3 != 0
+def vector_squares(n):
+    return n >= 20 and n % 3 != 0
 
 
 def tile_kanlinear_kernel(tc, x, base_w, base_b, spline_w, out):
@@ -49,40 +50,46 @@ def tile_kanlinear_kernel(tc, x, base_w, base_b, spline_w, out):
         ctx.enter_context(tc.manual_schedule())
         const = ctx.enter_context(tc.tile_pool(name="const", bufs=1))
         keep = ctx.enter_context(tc.tile_pool(name="keep", bufs=1))
-        chunks = ctx.enter_context(tc.tile_pool(name="chunks", bufs=3))
+        chunks = ctx.enter_context(tc.tile_pool(name="chunks", bufs=N_CHUNKS))
         wgrps = ctx.enter_context(tc.tile_pool(name="wgrps", bufs=4))
+        x4p = ctx.enter_context(tc.tile_pool(name="x4p", bufs=5))
         qpool = ctx.enter_context(tc.tile_pool(name="qpool", bufs=3))
+        mids = ctx.enter_context(tc.tile_pool(name="mids", bufs=2))
         bgrps = ctx.enter_context(tc.tile_pool(name="bgrps", bufs=3))
         accp = ctx.enter_context(tc.psum_pool(name="accp", bufs=4))
         wk = ctx.enter_context(tc.psum_pool(name="wk", bufs=4))
 
         chunk_words = {}
 
-        def load_chunk(i):
-            ch = chunks.tile([P, 8192], BF16, tag="chunk", name="chunk%d" % i)
+        def load_half(s):
+            i, half = divmod(s, 2)
+            ch = chunks.tile([P, 4096], BF16, tag="chunk", name="chunk%d" % s)
             src = base_w if i == 0 else sw[:, 1024 * (i - 1) : 1024 * i]
-            for half in range(2):
-                nc.sync.dma_start(
-                    out=ch[:, 4096 * half : 4096 * half + 4096].rearrange("p (n k) -> p n k", n=4),
-                    in_=src[HALF * half : HALF * half + HALF, :].rearrange("(n p) k -> p n k", p=P),
-                )
-            chunk_words[i] = ch[:].bitcast(F32)
+            nc.sync.dma_start(
+                out=ch[:].rearrange("p (n k) -> p n k", n=4),
+                in_=src[HALF * half : HALF * half + HALF, :].rearrange("(n p) k -> p n k", p=P),
+            )
+            chunk_words[s] = ch[:].bitcast(F32)
 
-        x4s = [keep.tile([P, 8192], BF16, name="x4_%d" % r) for r in range(2)]
+        x4s = {}
 
-        def load_x4(r, j0, j1):
-            w0, w1 = P * j0, P * j1
-            tw = x4s[r][:].bitcast(F32).rearrange("p (d w) -> p d w", d=4)
+        def load_x4(r, h):
+            t = x4p.tile([P, 2048], BF16, tag="x4", name="x4_%d_%d" % (r, h))
+            tw = t[:].bitcast(F32).rearrange("p (d w) -> p d w", d=4)
             for s in range(4):
                 nc.sync.dma_start(
-                    out=tw[s:P:4, :, w0:w1],
-                    in_=scr[r][:, w0:w1].rearrange("(d q) w -> q d w", q=32),
+                    out=tw[s:P:4, :, :],
+                    in_=scr[r][:, 256 * h : 256 * h + 256].rearrange("(d q) w -> q d w", q=32),
                 )
+            x4s[(r, h)] = t
 
         acts = {}
         ident_f = const.tile([P, P], F32)
         ident_b = const.tile([P, P], BF16)
         bias_bc = const.tile([P, OUT_F], BF16)
+        table_in = const.tile([P, 1], F32)
+        table_out = const.tile([P, 1], F32)
+        nc.vector.memset(table_in[:], 0.0)
         make_identity(nc, ident_b[:])
         make_identity(nc, ident_f[:])
         vals = const.tile([P, P], F32)
@@ -102,61 +109,88 @@ def tile_kanlinear_kernel(tc, x, base_w, base_b, spline_w, out):
         neg_mid_e = [per_partition("neg_mid%d" % e, -STEP, 2.0 - STEP / 2 + (STEP, -STEP)[e]) for e in range(2)]
         exp_bias = per_partition("exp_bias", 0.0, -CINV * CINV * STEP * STEP / 4)
 
-        def x_to_scratch(r):
-            for bnk in range(2):
-                xp = wk.tile([P, 1024], BF16, tag="wk", name="xp")
-                for j4 in range(4):
-                    for mm in range(2):
-                        c0 = IN_F * (2 * r + mm) + P * (4 * bnk + j4)
-                        nc.tensor.transpose(
-                            out=xp[:, 256 * j4 + P * mm : 256 * j4 + P * mm + P],
-                            in_=x_nat[:, c0 : c0 + P],
-                            identity=ident_b[:],
-                        )
-                nc.scalar.copy(out=xts[r][:, 1024 * bnk : 1024 * bnk + 1024], in_=xp[:])
-                nc.scalar.dma_start(
-                    out=scr[r][:, 512 * bnk : 512 * bnk + 512],
-                    in_=xts[r][:].bitcast(F32)[:, 512 * bnk : 512 * bnk + 512],
-                )
+        def x_to_scratch(r, j0, j1):
+            xp = wk.tile([P, 1024], BF16, tag="wk", name="xp")
+            for jt in range(j0, j1):
+                for mm in range(2):
+                    c0 = IN_F * (2 * r + mm) + P * jt
+                    nc.tensor.transpose(
+                        out=xp[:, 256 * (jt - j0) + P * mm : 256 * (jt - j0) + P * mm + P],
+                        in_=x_nat[:, c0 : c0 + P],
+                        identity=ident_b[:],
+                    )
+            xt = head.tile([P, 1024], BF16, tag="xt", bufs=2, name="xt")
+            nc.vector.tensor_copy(out=xt[:, 0 : 256 * (j1 - j0)], in_=xp[:, 0 : 256 * (j1 - j0)])
+            nc.sync.dma_start(out=scr[r][:, P * j0 : P * j1], in_=xt[:].bitcast(F32)[:, 0 : P * (j1 - j0)])
 
-        def silu(r):
+        reps = {}
+        xreps = {}
+
+        def replicate(pair):
+            rp = head.tile([P, 1024], BF16, name="rep%d" % pair)
+            nc.vector.tensor_copy(
+                out=rp[:].rearrange("p (m f s) -> p m f s", m=2, s=4),
+                in_=x_nat[:]
+                .rearrange("p (m i) -> p m i", m=4)[:, 0:2, P * pair : P * pair + P]
+                .unsqueeze(3)
+                .to_broadcast([P, 2, P, 4]),
+            )
+            reps[pair] = rp
+
+        def replicate_transposes(pair, pool, tag):
+            xr = pool.tile([P, 1024], BF16, tag=tag, name="xr")
+            for v in range(4):
+                for mm in range(2):
+                    c0 = 512 * mm + P * v
+                    nc.tensor.transpose(
+                        out=xr[:, 256 * v + P * mm : 256 * v + P * mm + P],
+                        in_=reps[pair][:, c0 : c0 + P],
+                        identity=ident_b[:],
+                    )
+            xreps[pair] = xr
+
+        sgrps = {}
+
+        def silu_transposes(r, g):
             x_words = x_nat[:].bitcast(F32)
-            for g in range(2):
-                sp = wk.tile([P, 512], F32, tag="wk", name="sp")
-                for u in range(2):
-                    for mm in range(2):
-                        c0 = 512 * (2 * r + mm) + 256 * g + P * u
-                        nc.tensor.transpose(
-                            out=sp[:, 256 * u + P * mm : 256 * u + P * mm + P],
-                            in_=x_words[:, c0 : c0 + P],
-                            identity=ident_f[:],
-                        )
-                grp = bgrps.tile([P, 4 * RH], BF16, align_bytes=64, tag="bgrp", name="sgrp")
-                nc.scalar.activation(
-                    out=grp[:].rearrange("p (r u e) -> p r u e", u=2, e=2),
-                    in_=sp[:].bitcast(BF16).rearrange("p (u r e) -> p r u e", u=2, e=2),
-                    func=ACT.Silu,
-                )
-                codes = keep.tile([P, RH], U32, align_bytes=64, name="sq_%d_%d" % (r, g))
-                plane = keep.tile([P, RH], U8, align_bytes=64, name="ss_%d_%d" % (r, g))
-                nc.vector.quantize_mx(out=codes[:].bitcast(FP8X4), scales=plane[:], in_=grp[:])
-                acts[(("b", g), r)] = (codes, plane)
+            sp = accp.tile([P, 512], F32, tag="acc", name="sp")
+            for u in range(2):
+                for mm in range(2):
+                    c0 = 512 * (2 * r + mm) + 256 * g + P * u
+                    nc.tensor.transpose(
+                        out=sp[:, 256 * u + P * mm : 256 * u + P * mm + P],
+                        in_=x_words[:, c0 : c0 + P],
+                        identity=ident_f[:],
+                    )
+            grp = head.tile([P, 4 * RH], BF16, align_bytes=64, tag="sgrp", bufs=2, name="sgrp")
+            nc.scalar.activation(
+                out=grp[:].rearrange("p (r u e) -> p r u e", u=2, e=2),
+                in_=sp[:].bitcast(BF16).rearrange("p (u r e) -> p r u e", u=2, e=2),
+                func=ACT.Silu,
+            )
+            sgrps[(r, g)] = grp
 
-        units = [(("b", g), half, 0) for half in range(2) for g in range(2)]
-        units += [(("s", c), half, 1 + c // 2) for c in range(16) for half in range(2)]
+        def silu_quantise(r, g):
+            codes = keep.tile([P, RH], U32, align_bytes=64, name="sq_%d_%d" % (r, g))
+            plane = keep.tile([P, RH], U8, align_bytes=64, name="ss_%d_%d" % (r, g))
+            nc.vector.quantize_mx(out=codes[:].bitcast(FP8X4), scales=plane[:], in_=sgrps[(r, g)][:])
+            acts[(("b", g), r)] = (codes, plane)
+
+        units = [(("b", g), half, half) for half in range(2) for g in range(2)]
+        units += [(("s", 2 * i + b), half, 2 + 2 * i + half) for i in range(8) for half in range(2) for b in range(2)]
         wgrp_of = {}
         banks = {}
         wts = {}
 
         def w_transposes(j, q):
-            kk, half, ci = units[j]
+            kk, half, s = units[j]
             wt = wk.tile([P, 512], F32, tag="wk", name="wt")
             for nn in range(2):
                 for u in range(2):
-                    c0 = 512 * (4 * half + 2 * q + nn) + 256 * (kk[1] % 2) + P * u
+                    c0 = 512 * (2 * q + nn) + 256 * (kk[1] % 2) + P * u
                     nc.tensor.transpose(
                         out=wt[:, 256 * nn + P * u : 256 * nn + P * u + P],
-                        in_=chunk_words[ci][:, c0 : c0 + P],
+                        in_=chunk_words[s][:, c0 : c0 + P],
                         identity=ident_f[:],
                     )
             banks[(j, q)] = wt
@@ -182,12 +216,17 @@ def tile_kanlinear_kernel(tc, x, base_w, base_b, spline_w, out):
         grp_of = {}
         qq_of = {}
 
-        def basis_squares(c, r, on_vector):
-            src = x4s[r][:].rearrange("p (d t r) -> p d t r", d=4, t=8)[:, 2 * (c % 2) : 2 * (c % 2) + 2, c // 2, :]
+        def basis_squares(n):
+            r, c = divmod(n, 16)
+            if n < N_DIRECT:
+                src = xreps[c // 2][:].rearrange("p (v r) -> p v r", v=4)[:, 2 * (c % 2) : 2 * (c % 2) + 2, :]
+            else:
+                x4 = x4s[(r, c // 4)][:].rearrange("p (d t r) -> p d t r", d=4, t=2)
+                src = x4[:, 2 * (c % 2) : 2 * (c % 2) + 2, c // 2 % 2, :]
             qq = qpool.tile([P, 4 * RH], F32, tag="qq", name="qq")
             qv = qq[:].rearrange("p (u e r) -> p u e r", u=2, e=2)
-            if on_vector:
-                mid = qpool.tile([P, 2 * RH], F32, tag="mid", name="mid")
+            if vector_squares(n):
+                mid = mids.tile([P, 2 * RH], F32, tag="mid", name="mid")
                 mv = mid[:].rearrange("p (u r) -> p u r", u=2)
                 nc.vector.tensor_scalar(out=mv, in0=src, scalar1=neg_mid[:, 0:1], scalar2=None, op0=ALU.add)
                 for e in range(2):
@@ -199,24 +238,23 @@ def tile_kanlinear_kernel(tc, x, base_w, base_b, spline_w, out):
                     nc.scalar.activation(
                         out=qv[:, :, e, :], in_=src, func=ACT.Square, bias=sq_bias[e][:, 0:1], scale=CINV
                     )
-            qq_of[(c, r)] = (qq, on_vector)
+            qq_of[n] = qq
 
-        def basis_exp(c, r):
-            qq, on_vector = qq_of[(c, r)]
+        def basis_exp(n):
             grp = bgrps.tile([P, 4 * RH], BF16, align_bytes=64, tag="bgrp", name="bgrp")
             dst = grp[:].rearrange("p (c i t) -> p c t i", i=4, t=4)
-            srcv = qq[:].rearrange("p (t c i) -> p c t i", i=4, t=4)
-            if on_vector:
+            srcv = qq_of[n][:].rearrange("p (t c i) -> p c t i", i=4, t=4)
+            if vector_squares(n):
                 nc.scalar.activation(out=dst, in_=srcv, func=ACT.Exp, bias=exp_bias[:, 0:1], scale=-CINV * CINV)
             else:
                 nc.scalar.activation(out=dst, in_=srcv, func=ACT.Exp, scale=-1.0)
-            grp_of[(c, r)] = grp
+            grp_of[n] = grp
 
-        def basis_quantise(c, r):
+        def basis_quantise(n):
             codes = bcp.tile([P, RH], U32, align_bytes=64, tag="codes", name="bq")
             plane = bcp.tile([P, RH], U8, align_bytes=64, tag="plane", name="bs")
-            nc.vector.quantize_mx(out=codes[:].bitcast(FP8X4), scales=plane[:], in_=grp_of[(c, r)][:])
-            acts[(("s", c), r)] = (codes, plane)
+            nc.vector.quantize_mx(out=codes[:].bitcast(FP8X4), scales=plane[:], in_=grp_of[n][:])
+            acts[(("s", n % 16), n // 16)] = (codes, plane)
 
         def mx_one(accs, kk, half, mm, r):
             a_c, a_p = acts[(kk, r)]
@@ -250,92 +288,107 @@ def tile_kanlinear_kernel(tc, x, base_w, base_b, spline_w, out):
             r0 = RH * r + P * mm
             nc.sync.dma_start(out=of[r0 : r0 + P, cols], in_=res[:])
 
-        accs = new_accs(accp, "acc")
+        accs = {}
 
         def step(s):
             pair = (2 * s, 2 * s + 1)
             for j in pair:
                 for q in range(2):
                     w_transposes(j, q)
+            if s == MX_LAG:
+                accs.update(new_accs(accp, "acc"))
             if s >= MX_LAG:
                 for j in pair:
                     mx(accs, j - 2 * MX_LAG, 0)
             w_evict(pair[0], 0)
             w_evict(pair[0], 1)
-            c = s - BASIS_AT
-            if c >= 0:
-                basis_squares(c, 0, False)
+            if s >= 1:
+                basis_squares(s + 1)
             w_evict(pair[1], 0)
             w_evict(pair[1], 1)
-            if c >= 1:
-                basis_exp(c - 1, 0)
-            if s % 2 == 1 and s // 2 + 3 <= 8:
-                load_chunk(s // 2 + 3)
-            if s == 12:
+            basis_exp(s)
+            if s + N_CHUNKS < N_STEPS:
+                load_half(s + N_CHUNKS)
+            if s in (9, 11, 13, 15):
+                load_x4(1, (s - 9) // 2)
+            if s == 14:
                 nc.sync.dma_start(out=bias_bc[:], in_=base_b.partition_broadcast(P))
-                load_x4(1, 0, 2)
-                load_x4(1, 2, 8)
+            if s == 0:
+                replicate_transposes(1, accp, "acc")
             if s == 1:
-                x_to_scratch(1)
-            if s == 2:
-                silu(1)
+                for g in range(2):
+                    silu_quantise(1, g)
+            if s == 5:
+                x_to_scratch(1, 0, 4)
+            if s == 6:
+                x_to_scratch(1, 4, 8)
             if s >= 1:
                 w_quantise(2 * s - 2)
                 w_quantise(2 * s - 1)
-            if c >= 2:
-                basis_quantise(c - 2, 0)
+            if s >= 1:
+                basis_quantise(s - 1)
 
+        bcp = ctx.enter_context(tc.tile_pool(name="bcp", bufs=7))
         with tc.tile_pool(name="head", bufs=1) as head:
             x_nat = head.tile([P, 4 * IN_F], BF16)
-            xts = [head.tile([P, 2048], BF16, name="xts%d" % r) for r in range(2)]
             for r in range(2):
                 nc.sync.dma_start(
                     out=x_nat[:, 2048 * r : 2048 * r + 2048].rearrange("p (m i) -> p m i", m=2),
                     in_=xf[RH * r : RH * r + RH, :].rearrange("(m p) i -> p m i", p=P),
                 )
-            for i in range(2):
-                load_chunk(i)
-            x_to_scratch(0)
-            load_x4(0, 0, 2)
-            load_x4(0, 2, 8)
-            load_chunk(2)
-            silu(0)
+            for s in range(3):
+                load_half(s)
+            nc.scalar.activation(out=table_out[:], in_=table_in[:], func=ACT.Silu)
+            for g in range(2):
+                silu_transposes(0, g)
+            replicate(0)
+            x_to_scratch(0, 2, 6)
+            x_to_scratch(0, 6, 8)
+            load_half(3)
+            replicate_transposes(0, wk, "wk")
+            replicate(1)
+            for g in range(2):
+                silu_quantise(0, g)
+            basis_squares(0)
+            basis_squares(1)
+            for g in range(2):
+                silu_transposes(1, g)
+            load_x4(0, 1)
+            load_half(4)
+            load_x4(0, 2)
+            load_x4(0, 3)
+            load_half(5)
             for s in range(HEAD_STEPS):
                 step(s)
-        bcp = ctx.enter_context(tc.tile_pool(name="bcp", bufs=8))
         ostage = ctx.enter_context(tc.tile_pool(name="ostage", bufs=4))
         for s in range(HEAD_STEPS, N_STEPS):
             step(s)
 
-        w_quantise(2 * N_STEPS - 2)
-        w_quantise(2 * N_STEPS - 1)
-        basis_exp(14, 0)
-        basis_quantise(13, 0)
-        basis_squares(15, 0, True)
-        basis_squares(0, 1, True)
-        basis_exp(15, 0)
-        basis_quantise(14, 0)
-        basis_squares(1, 1, True)
-        basis_exp(0, 1)
-        basis_quantise(15, 0)
-        for j in range(2 * (N_STEPS - MX_LAG), 2 * N_STEPS):
-            mx(accs, j, 0)
-        accs2 = new_accs(wk, "wk")
-        for j in range(4):
-            mx(accs2, j, 1)
-
-        for i in range(1, 17):
-            if i < 16:
-                if i + 1 < 16:
-                    basis_squares(i + 1, 1, vector_squares(i + 1))
-                basis_exp(i, 1)
-            basis_quantise(i - 1, 1)
-            if 3 <= i < 7:
-                finish(accs, 0, (i - 3) // 2, (i - 3) % 2)
-            if i <= 14:
-                for half in range(2):
-                    for mm in range(2):
-                        mx_one(accs2, ("s", i - 1), half, mm, 1)
+        accs2 = {}
+        for n in range(N_STEPS, 33):
+            if n == N_STEPS:
+                for j in (2 * n - 2, 2 * n - 1):
+                    w_quantise(j)
+            if n + 1 < 32:
+                basis_squares(n + 1)
+            if n < 32:
+                basis_exp(n)
+            basis_quantise(n - 1)
+            if n < N_STEPS + MX_LAG:
+                for j in (2 * n, 2 * n + 1):
+                    mx(accs, j - 2 * MX_LAG, 0)
+            if n == N_STEPS + MX_LAG:
+                accs2.update(new_accs(wk, "wk"))
+                for j in range(4):
+                    mx(accs2, j, 1)
+            if N_STEPS + MX_LAG <= n < N_STEPS + MX_LAG + 4:
+                finish(accs, 0, (n - N_STEPS - MX_LAG) // 2, (n - N_STEPS - MX_LAG) % 2)
+            first = 16 if n == N_STEPS + MX_LAG else n - 1
+            if n >= N_STEPS + MX_LAG:
+                for i in range(first, min(n, 30)):
+                    for half in range(2):
+                        for mm in range(2):
+                            mx_one(accs2, ("s", i - 16), half, mm, 1)
         for half in range(2):
             for mm in range(2):
                 for c in (14, 15):

@@ -26,7 +26,7 @@ FLOPS = 2 * ROWS * OUT_F * (IN_F + IN_F * GRID)
 
 N_STEPS = 18
 HEAD_STEPS = 8
-MX_LAG = 2
+MX_LAG = 3
 N_CHUNKS = 6
 N_DIRECT = 4
 
@@ -71,6 +71,12 @@ def tile_kanlinear_kernel(tc, x, base_w, base_b, spline_w, out):
             )
             chunk_words[s] = ch[:].bitcast(F32)
 
+        def load_x(r, cols):
+            nc.sync.dma_start(
+                out=x_nat[:, 2048 * r : 2048 * r + 2048].rearrange("p (m i) -> p m i", m=2)[:, :, cols],
+                in_=xf[RH * r : RH * r + RH, cols].rearrange("(m p) i -> p m i", p=P),
+            )
+
         x4s = {}
 
         def load_x4(r, h):
@@ -87,8 +93,10 @@ def tile_kanlinear_kernel(tc, x, base_w, base_b, spline_w, out):
         ident_f = const.tile([P, P], F32)
         ident_b = const.tile([P, P], BF16)
         bias_bc = const.tile([P, OUT_F], BF16)
+        zeros = const.tile([P, HALF], BF16)
         table_in = const.tile([P, 1], F32)
         table_out = const.tile([P, 1], F32)
+        nc.vector.memset(zeros[:], 0.0)
         nc.vector.memset(table_in[:], 0.0)
         make_identity(nc, ident_b[:])
         make_identity(nc, ident_f[:])
@@ -150,10 +158,14 @@ def tile_kanlinear_kernel(tc, x, base_w, base_b, spline_w, out):
             xreps[pair] = xr
 
         sgrps = {}
+        sps = {}
+
+        def silu_bank(r, g):
+            sps[(r, g)] = accp.tile([P, 512], F32, tag="acc", name="sp")
 
         def silu_transposes(r, g):
             x_words = x_nat[:].bitcast(F32)
-            sp = accp.tile([P, 512], F32, tag="acc", name="sp")
+            sp = sps[(r, g)]
             for u in range(2):
                 for mm in range(2):
                     c0 = 512 * (2 * r + mm) + 256 * g + P * u
@@ -216,19 +228,33 @@ def tile_kanlinear_kernel(tc, x, base_w, base_b, spline_w, out):
         grp_of = {}
         qq_of = {}
 
-        def basis_squares(n):
+        mid_of = {}
+
+        def basis_x(n):
             r, c = divmod(n, 16)
             if n < N_DIRECT:
-                src = xreps[c // 2][:].rearrange("p (v r) -> p v r", v=4)[:, 2 * (c % 2) : 2 * (c % 2) + 2, :]
-            else:
-                x4 = x4s[(r, c // 4)][:].rearrange("p (d t r) -> p d t r", d=4, t=2)
-                src = x4[:, 2 * (c % 2) : 2 * (c % 2) + 2, c // 2 % 2, :]
+                return xreps[c // 2][:].rearrange("p (v r) -> p v r", v=4)[:, 2 * (c % 2) : 2 * (c % 2) + 2, :]
+            x4 = x4s[(r, c // 4)][:].rearrange("p (d t r) -> p d t r", d=4, t=2)
+            return x4[:, 2 * (c % 2) : 2 * (c % 2) + 2, c // 2 % 2, :]
+
+        def basis_mid(n):
+            if vector_squares(n):
+                mid = mids.tile([P, 2 * RH], F32, tag="mid", name="mid")
+                nc.vector.tensor_scalar(
+                    out=mid[:].rearrange("p (u r) -> p u r", u=2),
+                    in0=basis_x(n),
+                    scalar1=neg_mid[:, 0:1],
+                    scalar2=None,
+                    op0=ALU.add,
+                )
+                mid_of[n] = mid
+
+        def basis_squares(n):
+            src = basis_x(n)
             qq = qpool.tile([P, 4 * RH], F32, tag="qq", name="qq")
             qv = qq[:].rearrange("p (u e r) -> p u e r", u=2, e=2)
             if vector_squares(n):
-                mid = mids.tile([P, 2 * RH], F32, tag="mid", name="mid")
-                mv = mid[:].rearrange("p (u r) -> p u r", u=2)
-                nc.vector.tensor_scalar(out=mv, in0=src, scalar1=neg_mid[:, 0:1], scalar2=None, op0=ALU.add)
+                mv = mid_of[n][:].rearrange("p (u r) -> p u r", u=2)
                 for e in range(2):
                     nc.vector.scalar_tensor_tensor(
                         out=qv[:, :, e, :], in0=src, scalar=neg_mid_e[e][:, 0:1], in1=mv, op0=ALU.add, op1=ALU.mult
@@ -290,16 +316,26 @@ def tile_kanlinear_kernel(tc, x, base_w, base_b, spline_w, out):
 
         accs = {}
 
+        def warm(count):
+            for i in range(count):
+                nc.tensor.matmul(out=idle_banks[0][:], lhsT=zeros[:, 0:P], rhs=zeros[:], start=True, stop=True)
+
+        idle_banks = []
+
         def step(s):
             pair = (2 * s, 2 * s + 1)
+            if s == MX_LAG:
+                accs.update(new_accs(accp, "acc"))
             for j in pair:
                 for q in range(2):
                     w_transposes(j, q)
-            if s == MX_LAG:
-                accs.update(new_accs(accp, "acc"))
-            if s >= MX_LAG:
-                for j in pair:
+                if s >= MX_LAG:
                     mx(accs, j - 2 * MX_LAG, 0)
+                else:
+                    warm(2)
+            if s == 0:
+                for g in range(2):
+                    silu_transposes(1, g)
             w_evict(pair[0], 0)
             w_evict(pair[0], 1)
             if s >= 1:
@@ -328,31 +364,35 @@ def tile_kanlinear_kernel(tc, x, base_w, base_b, spline_w, out):
             if s >= 1:
                 basis_quantise(s - 1)
 
-        bcp = ctx.enter_context(tc.tile_pool(name="bcp", bufs=7))
+        bcp = ctx.enter_context(tc.tile_pool(name="bcp", bufs=9))
         with tc.tile_pool(name="head", bufs=1) as head:
             x_nat = head.tile([P, 4 * IN_F], BF16)
-            for r in range(2):
-                nc.sync.dma_start(
-                    out=x_nat[:, 2048 * r : 2048 * r + 2048].rearrange("p (m i) -> p m i", m=2),
-                    in_=xf[RH * r : RH * r + RH, :].rearrange("(m p) i -> p m i", p=P),
-                )
+            for g in range(2):
+                load_x(0, slice(512 * g, 512 * g + 512))
+            load_x(1, slice(0, IN_F))
             for s in range(3):
                 load_half(s)
             nc.scalar.activation(out=table_out[:], in_=table_in[:], func=ACT.Silu)
+            for g in range(2):
+                silu_bank(0, g)
+            idle_banks.append(accp.tile([P, HALF], F32, tag="acc", name="idle"))
+            for g in range(2):
+                silu_bank(1, g)
+
+            warm(6)
             for g in range(2):
                 silu_transposes(0, g)
             replicate(0)
             x_to_scratch(0, 2, 6)
             x_to_scratch(0, 6, 8)
             load_half(3)
+            warm(2)
             replicate_transposes(0, wk, "wk")
             replicate(1)
             for g in range(2):
                 silu_quantise(0, g)
             basis_squares(0)
             basis_squares(1)
-            for g in range(2):
-                silu_transposes(1, g)
             load_x4(0, 1)
             load_half(4)
             load_x4(0, 2)
@@ -371,6 +411,8 @@ def tile_kanlinear_kernel(tc, x, base_w, base_b, spline_w, out):
                     w_quantise(j)
             if n + 1 < 32:
                 basis_squares(n + 1)
+            if n + 2 < 32:
+                basis_mid(n + 2)
             if n < 32:
                 basis_exp(n)
             basis_quantise(n - 1)

@@ -186,7 +186,8 @@ def tile_kanlinear_kernel(tc, x, base_w, base_b, spline_w, out):
             codes = keep.tile([P, RH], U32, align_bytes=64, name="sq_%d_%d" % (r, g))
             plane = keep.tile([P, RH], U8, align_bytes=64, name="ss_%d_%d" % (r, g))
             nc.vector.quantize_mx(out=codes[:].bitcast(FP8X4), scales=plane[:], in_=sgrps[(r, g)][:])
-            acts[(("b", g), r)] = (codes, plane)
+            for mm in range(2):
+                acts[(("b", g), r, mm)] = (codes, plane, P * mm)
 
         units = [(("b", g), half, half) for half in range(2) for g in range(2)]
         units += [(("s", 2 * i + b), half, 2 + 2 * i + half) for i in range(8) for half in range(2) for b in range(2)]
@@ -230,31 +231,35 @@ def tile_kanlinear_kernel(tc, x, base_w, base_b, spline_w, out):
 
         mid_of = {}
 
-        def basis_x(n):
+        def basis_x(n, mm):
             r, c = divmod(n, 16)
             if n < N_DIRECT:
                 return xreps[c // 2][:].rearrange("p (v r) -> p v r", v=4)[:, 2 * (c % 2) : 2 * (c % 2) + 2, :]
             x4 = x4s[(r, c // 4)][:].rearrange("p (d t r) -> p d t r", d=4, t=2)
-            return x4[:, 2 * (c % 2) : 2 * (c % 2) + 2, c // 2 % 2, :]
+            rows = slice(0, RH) if mm is None else slice(P * mm, P * mm + P)
+            return x4[:, 2 * (c % 2) : 2 * (c % 2) + 2, c // 2 % 2, rows]
 
-        def basis_mid(n):
+        def n_rows(mm):
+            return RH if mm is None else P
+
+        def basis_mid(n, mm=None):
             if vector_squares(n):
                 mid = mids.tile([P, 2 * RH], F32, tag="mid", name="mid")
                 nc.vector.tensor_scalar(
-                    out=mid[:].rearrange("p (u r) -> p u r", u=2),
-                    in0=basis_x(n),
+                    out=mid[:, 0 : 2 * n_rows(mm)].rearrange("p (u r) -> p u r", u=2),
+                    in0=basis_x(n, mm),
                     scalar1=neg_mid[:, 0:1],
                     scalar2=None,
                     op0=ALU.add,
                 )
-                mid_of[n] = mid
+                mid_of[(n, mm)] = mid
 
-        def basis_squares(n):
-            src = basis_x(n)
+        def basis_squares(n, mm=None):
+            src = basis_x(n, mm)
             qq = qpool.tile([P, 4 * RH], F32, tag="qq", name="qq")
-            qv = qq[:].rearrange("p (u e r) -> p u e r", u=2, e=2)
+            qv = qq[:, 0 : 4 * n_rows(mm)].rearrange("p (u e r) -> p u e r", u=2, e=2)
             if vector_squares(n):
-                mv = mid_of[n][:].rearrange("p (u r) -> p u r", u=2)
+                mv = mid_of[(n, mm)][:, 0 : 2 * n_rows(mm)].rearrange("p (u r) -> p u r", u=2)
                 for e in range(2):
                     nc.vector.scalar_tensor_tensor(
                         out=qv[:, :, e, :], in0=src, scalar=neg_mid_e[e][:, 0:1], in1=mv, op0=ALU.add, op1=ALU.mult
@@ -264,31 +269,36 @@ def tile_kanlinear_kernel(tc, x, base_w, base_b, spline_w, out):
                     nc.scalar.activation(
                         out=qv[:, :, e, :], in_=src, func=ACT.Square, bias=sq_bias[e][:, 0:1], scale=CINV
                     )
-            qq_of[n] = qq
+            qq_of[(n, mm)] = qq
 
-        def basis_exp(n):
+        def basis_exp(n, mm=None):
             grp = bgrps.tile([P, 4 * RH], BF16, align_bytes=64, tag="bgrp", name="bgrp")
-            dst = grp[:].rearrange("p (c i t) -> p c t i", i=4, t=4)
-            srcv = qq_of[n][:].rearrange("p (t c i) -> p c t i", i=4, t=4)
+            width = 4 * n_rows(mm)
+            dst = grp[:, 0:width].rearrange("p (c i t) -> p c t i", i=4, t=4)
+            srcv = qq_of[(n, mm)][:, 0:width].rearrange("p (t c i) -> p c t i", i=4, t=4)
             if vector_squares(n):
                 nc.scalar.activation(out=dst, in_=srcv, func=ACT.Exp, bias=exp_bias[:, 0:1], scale=-CINV * CINV)
             else:
                 nc.scalar.activation(out=dst, in_=srcv, func=ACT.Exp, scale=-1.0)
-            grp_of[n] = grp
+            grp_of[(n, mm)] = grp
 
-        def basis_quantise(n):
+        def basis_quantise(n, mm=None):
+            w = n_rows(mm)
             codes = bcp.tile([P, RH], U32, align_bytes=64, tag="codes", name="bq")
             plane = bcp.tile([P, RH], U8, align_bytes=64, tag="plane", name="bs")
-            nc.vector.quantize_mx(out=codes[:].bitcast(FP8X4), scales=plane[:], in_=grp_of[n][:])
-            acts[(("s", n % 16), n // 16)] = (codes, plane)
+            nc.vector.quantize_mx(
+                out=codes[:, 0:w].bitcast(FP8X4), scales=plane[:, 0:w], in_=grp_of[(n, mm)][:, 0 : 4 * w]
+            )
+            for i in range(w // P):
+                acts[(("s", n % 16), n // 16, mm or i)] = (codes, plane, P * i)
 
         def mx_one(accs, kk, half, mm, r):
-            a_c, a_p = acts[(kk, r)]
+            a_c, a_p, r0 = acts[(kk, r, mm)]
             w_c, w_p = wts[(kk, half)]
             nc.tensor.matmul_mx(
                 out=accs[(mm, half)][:],
-                lhsT=a_c[:, P * mm : P * mm + P].bitcast(FP8X4),
-                lhsT_scale=a_p[:, P * mm : P * mm + P],
+                lhsT=a_c[:, r0 : r0 + P].bitcast(FP8X4),
+                lhsT_scale=a_p[:, r0 : r0 + P],
                 rhs=w_c[:].bitcast(FP8X4),
                 rhs_scale=w_p[:],
                 start=(kk == ("b", 0)),
@@ -333,9 +343,6 @@ def tile_kanlinear_kernel(tc, x, base_w, base_b, spline_w, out):
                     mx(accs, j - 2 * MX_LAG, 0)
                 else:
                     warm(2)
-            if s == 0:
-                for g in range(2):
-                    silu_transposes(1, g)
             w_evict(pair[0], 0)
             w_evict(pair[0], 1)
             if s >= 1:
@@ -379,7 +386,7 @@ def tile_kanlinear_kernel(tc, x, base_w, base_b, spline_w, out):
             for g in range(2):
                 silu_bank(1, g)
 
-            warm(6)
+            warm(3)
             for g in range(2):
                 silu_transposes(0, g)
             replicate(0)
@@ -393,6 +400,8 @@ def tile_kanlinear_kernel(tc, x, base_w, base_b, spline_w, out):
                 silu_quantise(0, g)
             basis_squares(0)
             basis_squares(1)
+            for g in range(2):
+                silu_transposes(1, g)
             load_x4(0, 1)
             load_half(4)
             load_x4(0, 2)
@@ -405,34 +414,44 @@ def tile_kanlinear_kernel(tc, x, base_w, base_b, spline_w, out):
             step(s)
 
         accs2 = {}
-        for n in range(N_STEPS, 33):
-            if n == N_STEPS:
-                for j in (2 * n - 2, 2 * n - 1):
+        items = [(n, None) for n in range(N_STEPS, 30)] + [(n, mm) for mm in range(2) for n in (30, 31)]
+        for k in range(len(items) + 1):
+            if k == 0:
+                for j in (2 * N_STEPS - 2, 2 * N_STEPS - 1):
                     w_quantise(j)
-            if n + 1 < 32:
-                basis_squares(n + 1)
-            if n + 2 < 32:
-                basis_mid(n + 2)
-            if n < 32:
-                basis_exp(n)
-            basis_quantise(n - 1)
-            if n < N_STEPS + MX_LAG:
-                for j in (2 * n, 2 * n + 1):
-                    mx(accs, j - 2 * MX_LAG, 0)
-            if n == N_STEPS + MX_LAG:
+            if k + 1 < len(items):
+                basis_squares(*items[k + 1])
+            if k + 2 < len(items):
+                basis_mid(*items[k + 2])
+            if k < len(items):
+                basis_exp(*items[k])
+            if k == 0:
+                basis_quantise(N_STEPS - 1)
+            else:
+                basis_quantise(*items[k - 1])
+            if k < MX_LAG:
+                for j in (2 * (N_STEPS + k - MX_LAG), 2 * (N_STEPS + k - MX_LAG) + 1):
+                    mx(accs, j, 0)
+            if k == MX_LAG:
                 accs2.update(new_accs(wk, "wk"))
                 for j in range(4):
                     mx(accs2, j, 1)
-            if N_STEPS + MX_LAG <= n < N_STEPS + MX_LAG + 4:
-                finish(accs, 0, (n - N_STEPS - MX_LAG) // 2, (n - N_STEPS - MX_LAG) % 2)
-            first = 16 if n == N_STEPS + MX_LAG else n - 1
-            if n >= N_STEPS + MX_LAG:
-                for i in range(first, min(n, 30)):
+                for n in range(16, N_STEPS + k - 1):
                     for half in range(2):
                         for mm in range(2):
-                            mx_one(accs2, ("s", i - 16), half, mm, 1)
-        for half in range(2):
-            for mm in range(2):
-                for c in (14, 15):
-                    mx_one(accs2, ("s", c), half, mm, 1)
+                            mx_one(accs2, ("s", n - 16), half, mm, 1)
+            if MX_LAG <= k < MX_LAG + 4:
+                finish(accs, 0, (k - MX_LAG) // 2, (k - MX_LAG) % 2)
+            if k >= MX_LAG:
+                n, part = items[k - 1]
+                if part is None:
+                    for half in range(2):
+                        for mm in range(2):
+                            mx_one(accs2, ("s", n - 16), half, mm, 1)
+                elif n == 31:
+                    for half in range(2):
+                        for c in (14, 15):
+                            mx_one(accs2, ("s", c), half, part, 1)
+        for mm in range(2):
+            for half in range(2):
                 finish(accs2, 1, half, mm)

@@ -27,7 +27,7 @@ FLOPS = 2 * ROWS * OUT_F * (IN_F + IN_F * GRID)
 N_STEPS = 18
 HEAD_STEPS = 8
 MX_LAG = 3
-N_CHUNKS = 6
+N_CHUNKS = 3
 N_DIRECT = 4
 
 
@@ -52,24 +52,30 @@ def tile_kanlinear_kernel(tc, x, base_w, base_b, spline_w, out):
         keep = ctx.enter_context(tc.tile_pool(name="keep", bufs=1))
         chunks = ctx.enter_context(tc.tile_pool(name="chunks", bufs=N_CHUNKS))
         wgrps = ctx.enter_context(tc.tile_pool(name="wgrps", bufs=4))
-        x4p = ctx.enter_context(tc.tile_pool(name="x4p", bufs=5))
+        x4p = ctx.enter_context(tc.tile_pool(name="x4p", bufs=3))
         qpool = ctx.enter_context(tc.tile_pool(name="qpool", bufs=3))
         mids = ctx.enter_context(tc.tile_pool(name="mids", bufs=2))
         bgrps = ctx.enter_context(tc.tile_pool(name="bgrps", bufs=3))
         accp = ctx.enter_context(tc.psum_pool(name="accp", bufs=4))
         wk = ctx.enter_context(tc.psum_pool(name="wk", bufs=4))
 
+        chunk_of = {}
         chunk_words = {}
 
-        def load_half(s):
-            i, half = divmod(s, 2)
-            ch = chunks.tile([P, 4096], BF16, tag="chunk", name="chunk%d" % s)
-            src = base_w if i == 0 else sw[:, 1024 * (i - 1) : 1024 * i]
-            nc.sync.dma_start(
-                out=ch[:].rearrange("p (n k) -> p n k", n=4),
-                in_=src[HALF * half : HALF * half + HALF, :].rearrange("(n p) k -> p n k", p=P),
-            )
-            chunk_words[s] = ch[:].bitcast(F32)
+        def load_chunk(i, parts=(0, 1)):
+            if 0 in parts:
+                chunk_of[i] = chunks.tile([P, 8192], BF16, tag="chunk", name="chunk%d" % i)
+            ch = chunk_of[i]
+            region, half = divmod(i - 1, 2)
+            n_tiles = 8 if i == 0 else 4
+            src = base_w if i == 0 else sw[HALF * half : HALF * half + HALF, 2048 * region : 2048 * region + 2048]
+            for part in parts:
+                rows = slice(P * n_tiles // 2 * part, P * n_tiles // 2 * (part + 1))
+                nc.sync.dma_start(
+                    out=ch[:, 4096 * part : 4096 * part + 4096].rearrange("p (n k) -> p n k", n=n_tiles // 2),
+                    in_=src[rows, :].rearrange("(n p) k -> p n k", p=P),
+                )
+            chunk_words[i] = ch[:].bitcast(F32)
 
         def load_x(r, cols):
             nc.sync.dma_start(
@@ -80,19 +86,19 @@ def tile_kanlinear_kernel(tc, x, base_w, base_b, spline_w, out):
         x4s = {}
 
         def load_x4(r, h):
-            t = x4p.tile([P, 2048], BF16, tag="x4", name="x4_%d_%d" % (r, h))
+            t = x4p.tile([P, 4096], BF16, tag="x4", name="x4_%d_%d" % (r, h))
             tw = t[:].bitcast(F32).rearrange("p (d w) -> p d w", d=4)
+            w0 = 256 if (r, h) == (0, 0) else 0
             for s in range(4):
                 nc.sync.dma_start(
-                    out=tw[s:P:4, :, :],
-                    in_=scr[r][:, 256 * h : 256 * h + 256].rearrange("(d q) w -> q d w", q=32),
+                    out=tw[s:P:4, :, w0:512],
+                    in_=scr[r][:, 512 * h + w0 : 512 * h + 512].rearrange("(d q) w -> q d w", q=32),
                 )
             x4s[(r, h)] = t
 
         acts = {}
         ident_f = const.tile([P, P], F32)
         ident_b = const.tile([P, P], BF16)
-        bias_bc = const.tile([P, OUT_F], BF16)
         zeros = const.tile([P, HALF], BF16)
         table_in = const.tile([P, 1], F32)
         table_out = const.tile([P, 1], F32)
@@ -135,7 +141,7 @@ def tile_kanlinear_kernel(tc, x, base_w, base_b, spline_w, out):
         xreps = {}
 
         def replicate(pair):
-            rp = head.tile([P, 1024], BF16, name="rep%d" % pair)
+            rp = head.tile([P, 1024], BF16, tag="rep", name="rep")
             nc.vector.tensor_copy(
                 out=rp[:].rearrange("p (m f s) -> p m f s", m=2, s=4),
                 in_=x_nat[:]
@@ -189,21 +195,22 @@ def tile_kanlinear_kernel(tc, x, base_w, base_b, spline_w, out):
             for mm in range(2):
                 acts[(("b", g), r, mm)] = (codes, plane, P * mm)
 
-        units = [(("b", g), half, half) for half in range(2) for g in range(2)]
-        units += [(("s", 2 * i + b), half, 2 + 2 * i + half) for i in range(8) for half in range(2) for b in range(2)]
+        units = [(("b", g), half, 0) for half in range(2) for g in range(2)]
+        units += [(("s", 4 * i + b), half, 1 + 2 * i + half) for i in range(4) for half in range(2) for b in range(4)]
         wgrp_of = {}
         banks = {}
         wts = {}
 
         def w_transposes(j, q):
-            kk, half, s = units[j]
+            kk, half, ci = units[j]
             wt = wk.tile([P, 512], F32, tag="wk", name="wt")
             for nn in range(2):
                 for u in range(2):
-                    c0 = 512 * (2 * q + nn) + 256 * (kk[1] % 2) + P * u
+                    n = 2 * q + nn
+                    c0 = (512 * (4 * half + n) if ci == 0 else 1024 * n) + 256 * kk[1] % 1024 + P * u
                     nc.tensor.transpose(
                         out=wt[:, 256 * nn + P * u : 256 * nn + P * u + P],
-                        in_=chunk_words[s][:, c0 : c0 + P],
+                        in_=chunk_words[ci][:, c0 : c0 + P],
                         identity=ident_f[:],
                     )
             banks[(j, q)] = wt
@@ -235,9 +242,9 @@ def tile_kanlinear_kernel(tc, x, base_w, base_b, spline_w, out):
             r, c = divmod(n, 16)
             if n < N_DIRECT:
                 return xreps[c // 2][:].rearrange("p (v r) -> p v r", v=4)[:, 2 * (c % 2) : 2 * (c % 2) + 2, :]
-            x4 = x4s[(r, c // 4)][:].rearrange("p (d t r) -> p d t r", d=4, t=2)
+            x4 = x4s[(r, c // 8)][:].rearrange("p (d t r) -> p d t r", d=4, t=4)
             rows = slice(0, RH) if mm is None else slice(P * mm, P * mm + P)
-            return x4[:, 2 * (c % 2) : 2 * (c % 2) + 2, c // 2 % 2, rows]
+            return x4[:, 2 * (c % 2) : 2 * (c % 2) + 2, c // 2 % 4, rows]
 
         def n_rows(mm):
             return RH if mm is None else P
@@ -343,6 +350,9 @@ def tile_kanlinear_kernel(tc, x, base_w, base_b, spline_w, out):
                     mx(accs, j - 2 * MX_LAG, 0)
                 else:
                     warm(2)
+                if j == 0:
+                    for g in range(2):
+                        silu_transposes(1, g)
             w_evict(pair[0], 0)
             w_evict(pair[0], 1)
             if s >= 1:
@@ -350,11 +360,13 @@ def tile_kanlinear_kernel(tc, x, base_w, base_b, spline_w, out):
             w_evict(pair[1], 0)
             w_evict(pair[1], 1)
             basis_exp(s)
-            if s + N_CHUNKS < N_STEPS:
-                load_half(s + N_CHUNKS)
-            if s in (9, 11, 13, 15):
-                load_x4(1, (s - 9) // 2)
-            if s == 14:
+            if s % 2 == 1 and s // 2 + N_CHUNKS < 9:
+                load_chunk(s // 2 + N_CHUNKS)
+            if s == 3:
+                load_x4(0, 1)
+            if s in (10, 14):
+                load_x4(1, (s - 10) // 4)
+            if s == 16:
                 nc.sync.dma_start(out=bias_bc[:], in_=base_b.partition_broadcast(P))
             if s == 0:
                 replicate_transposes(1, accp, "acc")
@@ -376,9 +388,10 @@ def tile_kanlinear_kernel(tc, x, base_w, base_b, spline_w, out):
             x_nat = head.tile([P, 4 * IN_F], BF16)
             for g in range(2):
                 load_x(0, slice(512 * g, 512 * g + 512))
+            load_chunk(0, (0,))
             load_x(1, slice(0, IN_F))
-            for s in range(3):
-                load_half(s)
+            load_chunk(0, (1,))
+            load_chunk(1, (0,))
             nc.scalar.activation(out=table_out[:], in_=table_in[:], func=ACT.Silu)
             for g in range(2):
                 silu_bank(0, g)
@@ -392,7 +405,7 @@ def tile_kanlinear_kernel(tc, x, base_w, base_b, spline_w, out):
             replicate(0)
             x_to_scratch(0, 2, 6)
             x_to_scratch(0, 6, 8)
-            load_half(3)
+            load_chunk(1, (1,))
             warm(2)
             replicate_transposes(0, wk, "wk")
             replicate(1)
@@ -400,16 +413,13 @@ def tile_kanlinear_kernel(tc, x, base_w, base_b, spline_w, out):
                 silu_quantise(0, g)
             basis_squares(0)
             basis_squares(1)
-            for g in range(2):
-                silu_transposes(1, g)
-            load_x4(0, 1)
-            load_half(4)
-            load_x4(0, 2)
-            load_x4(0, 3)
-            load_half(5)
+            load_x4(0, 0)
+            load_chunk(2)
             for s in range(HEAD_STEPS):
                 step(s)
         ostage = ctx.enter_context(tc.tile_pool(name="ostage", bufs=4))
+        late = ctx.enter_context(tc.tile_pool(name="late", bufs=1))
+        bias_bc = late.tile([P, OUT_F], BF16)
         for s in range(HEAD_STEPS, N_STEPS):
             step(s)
 

@@ -27,12 +27,13 @@ FLOPS = 2 * ROWS * OUT_F * (IN_F + IN_F * GRID)
 N_STEPS = 18
 HEAD_STEPS = 8
 MX_LAG = 3
+MX_RUN_LAG = 5
 N_CHUNKS = 3
 N_DIRECT = 4
 
 
 def act_evicts(s, b):
-    return s >= 2 and (b == 1 or (b == 3 and s % 3 == 2))
+    return s >= 2 and (b == 1 or (b == 3 and s < 12 and s % 2 == 1))
 
 
 def vector_squares(n):
@@ -51,9 +52,9 @@ def tile_kanlinear_kernel(tc, x, base_w, base_b, spline_w, out):
         const = ctx.enter_context(tc.tile_pool(name="const", bufs=1))
         keep = ctx.enter_context(tc.tile_pool(name="keep", bufs=1))
         chunks = ctx.enter_context(tc.tile_pool(name="chunks", bufs=N_CHUNKS))
-        wgrps = ctx.enter_context(tc.tile_pool(name="wgrps", bufs=4))
-        x4p = ctx.enter_context(tc.tile_pool(name="x4p", bufs=3))
-        qpool = ctx.enter_context(tc.tile_pool(name="qpool", bufs=3))
+        wgrps = ctx.enter_context(tc.tile_pool(name="wgrps", bufs=2))
+        x4p = ctx.enter_context(tc.tile_pool(name="x4p", bufs=2))
+        qpool = ctx.enter_context(tc.tile_pool(name="qpool", bufs=4))
         mids = ctx.enter_context(tc.tile_pool(name="mids", bufs=2))
         bgrps = ctx.enter_context(tc.tile_pool(name="bgrps", bufs=3))
         accp = ctx.enter_context(tc.psum_pool(name="accp", bufs=4))
@@ -63,17 +64,16 @@ def tile_kanlinear_kernel(tc, x, base_w, base_b, spline_w, out):
         chunk_words = {}
 
         def load_chunk(i, parts=(0, 1)):
-            if 0 in parts:
+            if i not in chunk_of:
                 chunk_of[i] = chunks.tile([P, 8192], BF16, tag="chunk", name="chunk%d" % i)
             ch = chunk_of[i]
             region, half = divmod(i - 1, 2)
-            n_tiles = 8 if i == 0 else 4
             src = base_w if i == 0 else sw[HALF * half : HALF * half + HALF, 2048 * region : 2048 * region + 2048]
             for part in parts:
-                rows = slice(P * n_tiles // 2 * part, P * n_tiles // 2 * (part + 1))
+                width = 2048 if i == 0 else 4096
                 nc.sync.dma_start(
-                    out=ch[:, 4096 * part : 4096 * part + 4096].rearrange("p (n k) -> p n k", n=n_tiles // 2),
-                    in_=src[rows, :].rearrange("(n p) k -> p n k", p=P),
+                    out=ch[:, width * part : width * part + width].rearrange("p (n k) -> p n k", n=2),
+                    in_=src[2 * P * part : 2 * P * part + 2 * P, :].rearrange("(n p) k -> p n k", p=P),
                 )
             chunk_words[i] = ch[:].bitcast(F32)
 
@@ -141,7 +141,7 @@ def tile_kanlinear_kernel(tc, x, base_w, base_b, spline_w, out):
         xreps = {}
 
         def replicate(pair):
-            rp = head.tile([P, 1024], BF16, tag="rep", name="rep")
+            rp = head.tile([P, 1024], BF16, tag="rep", bufs=2, name="rep")
             nc.vector.tensor_copy(
                 out=rp[:].rearrange("p (m f s) -> p m f s", m=2, s=4),
                 in_=x_nat[:]
@@ -201,9 +201,10 @@ def tile_kanlinear_kernel(tc, x, base_w, base_b, spline_w, out):
         banks = {}
         wts = {}
 
-        def w_transposes(j, q):
+        def w_transposes(j, q, n_warm=0):
             kk, half, ci = units[j]
             wt = wk.tile([P, 512], F32, tag="wk", name="wt")
+            warm(n_warm, wt)
             for nn in range(2):
                 for u in range(2):
                     n = 2 * q + nn
@@ -216,22 +217,24 @@ def tile_kanlinear_kernel(tc, x, base_w, base_b, spline_w, out):
             banks[(j, q)] = wt
 
         def w_evict(j, q):
-            if q == 0:
-                wgrp_of[j] = wgrps.tile([P, 4 * HALF], BF16, align_bytes=64, tag="wgrp", name="wgrp")
-            dst = wgrp_of[j][:].bitcast(F32)[:, 512 * q : 512 * q + 512].rearrange("p (n o u) -> p n o u", n=2, u=2)
+            if j % 2 == 0 and q == 0:
+                wgrp_of[j // 2] = wgrps.tile([P, 8 * HALF], BF16, align_bytes=64, tag="wgrp", name="wgrp")
+            c0 = 1024 * (j % 2) + 512 * q
+            dst = wgrp_of[j // 2][:].bitcast(F32)[:, c0 : c0 + 512].rearrange("p (n o u) -> p n o u", n=2, u=2)
             srcv = banks[(j, q)][:].rearrange("p (n u o) -> p n o u", n=2, u=2)
-            if act_evicts(j // 2, 2 * (j % 2) + q):
+            if act_evicts(j // 2, 2 * q + j % 2):
                 nc.scalar.copy(out=dst, in_=srcv)
             else:
                 nc.vector.tensor_copy(out=dst, in_=srcv)
 
-        def w_quantise(j):
-            kk, half, ci = units[j]
-            nm = "%s%d_%d" % (kk[0], kk[1], half)
-            codes = keep.tile([P, HALF], U32, align_bytes=64, name="wq_" + nm)
-            plane = keep.tile([P, HALF], U8, align_bytes=64, name="ws_" + nm)
-            nc.vector.quantize_mx(out=codes[:].bitcast(FP8X4), scales=plane[:], in_=wgrp_of[j][:])
-            wts[(kk, half)] = (codes, plane)
+        def w_quantise(s):
+            codes = keep.tile([P, 2 * HALF], U32, align_bytes=64, name="wq_%d" % s)
+            plane = keep.tile([P, 2 * HALF], U8, align_bytes=64, name="ws_%d" % s)
+            nc.vector.quantize_mx(out=codes[:].bitcast(FP8X4), scales=plane[:], in_=wgrp_of[s][:])
+            for i in range(2):
+                kk, half, ci = units[2 * s + i]
+                cols = slice(HALF * i, HALF * i + HALF)
+                wts[(kk, half)] = (codes[:, cols], plane[:, cols])
 
         grp_of = {}
         qq_of = {}
@@ -306,8 +309,8 @@ def tile_kanlinear_kernel(tc, x, base_w, base_b, spline_w, out):
                 out=accs[(mm, half)][:],
                 lhsT=a_c[:, r0 : r0 + P].bitcast(FP8X4),
                 lhsT_scale=a_p[:, r0 : r0 + P],
-                rhs=w_c[:].bitcast(FP8X4),
-                rhs_scale=w_p[:],
+                rhs=w_c.bitcast(FP8X4),
+                rhs_scale=w_p,
                 start=(kk == ("b", 0)),
                 stop=(kk == ("s", 15)),
             )
@@ -332,55 +335,63 @@ def tile_kanlinear_kernel(tc, x, base_w, base_b, spline_w, out):
             nc.sync.dma_start(out=of[r0 : r0 + P, cols], in_=res[:])
 
         accs = {}
+        WARM = {0: 2, 1: 2, 2: 2, 3: 2, 4: 2, 5: 2}
 
-        def warm(count):
+        def warm(count, bank):
             for i in range(count):
-                nc.tensor.matmul(out=idle_banks[0][:], lhsT=zeros[:, 0:P], rhs=zeros[:], start=True, stop=True)
-
-        idle_banks = []
+                nc.tensor.matmul(out=bank[:], lhsT=zeros[:, 0:P], rhs=zeros[:], start=True, stop=True)
 
         def step(s):
             pair = (2 * s, 2 * s + 1)
-            if s == MX_LAG:
-                accs.update(new_accs(accp, "acc"))
-            for j in pair:
-                for q in range(2):
-                    w_transposes(j, q)
-                if s >= MX_LAG:
-                    mx(accs, j - 2 * MX_LAG, 0)
-                else:
-                    warm(2)
-                if j == 0:
+            for q in range(2):
+                run = 2 * s + q
+                if run == MX_RUN_LAG:
+                    accs.update(new_accs(accp, "acc"))
+                for j in pair:
+                    w_transposes(j, q, WARM.get(run, 0) if j == 2 * s else 0)
+                if run == 2:
                     for g in range(2):
+                        silu_bank(1, g)
                         silu_transposes(1, g)
-            w_evict(pair[0], 0)
-            w_evict(pair[0], 1)
+                if run >= MX_RUN_LAG:
+                    mx(accs, run - MX_RUN_LAG, 0)
+            for j in pair:
+                w_evict(j, 0)
             if s >= 1:
+                w_quantise(s - 1)
+            if s >= 3:
                 basis_squares(s + 1)
-            w_evict(pair[1], 0)
-            w_evict(pair[1], 1)
-            basis_exp(s)
-            if s % 2 == 1 and s // 2 + N_CHUNKS < 9:
-                load_chunk(s // 2 + N_CHUNKS)
-            if s == 3:
-                load_x4(0, 1)
-            if s in (10, 14):
-                load_x4(1, (s - 10) // 4)
-            if s == 16:
-                nc.sync.dma_start(out=bias_bc[:], in_=base_b.partition_broadcast(P))
-            if s == 0:
-                replicate_transposes(1, accp, "acc")
+            for j in pair:
+                w_evict(j, 1)
             if s == 1:
+                basis_exp(0)
+            if s >= 1:
+                basis_exp(s)
+            if s == 0:
+                x_to_scratch(0, 2, 6)
+                load_chunk(1, (1,))
+            if s == 0:
+                x_to_scratch(0, 6, 8)
+                load_x4(0, 0)
+                load_chunk(2)
+            if s == 4:
                 for g in range(2):
                     silu_quantise(1, g)
+            if s == 3:
+                load_x4(0, 1)
+            if s % 2 == 1 and s // 2 + N_CHUNKS < 9:
+                load_chunk(s // 2 + N_CHUNKS)
+            if s in (10, 15):
+                load_x4(1, (10, 15).index(s))
+            if s == 16:
+                nc.sync.dma_start(out=bias_bc[:], in_=base_b.partition_broadcast(P))
             if s == 5:
                 x_to_scratch(1, 0, 4)
             if s == 6:
                 x_to_scratch(1, 4, 8)
-            if s >= 1:
-                w_quantise(2 * s - 2)
-                w_quantise(2 * s - 1)
-            if s >= 1:
+            if s == 2:
+                basis_quantise(0)
+            if s >= 2:
                 basis_quantise(s - 1)
 
         bcp = ctx.enter_context(tc.tile_pool(name="bcp", bufs=9))
@@ -388,33 +399,25 @@ def tile_kanlinear_kernel(tc, x, base_w, base_b, spline_w, out):
             x_nat = head.tile([P, 4 * IN_F], BF16)
             for g in range(2):
                 load_x(0, slice(512 * g, 512 * g + 512))
-            load_chunk(0, (0,))
+            load_chunk(0, range(3))
             load_x(1, slice(0, IN_F))
-            load_chunk(0, (1,))
+            load_chunk(0, range(3, 4))
             load_chunk(1, (0,))
             nc.scalar.activation(out=table_out[:], in_=table_in[:], func=ACT.Silu)
             for g in range(2):
                 silu_bank(0, g)
-            idle_banks.append(accp.tile([P, HALF], F32, tag="acc", name="idle"))
-            for g in range(2):
-                silu_bank(1, g)
-
-            warm(3)
-            for g in range(2):
-                silu_transposes(0, g)
+            warm(3, sps[(0, 0)])
+            silu_transposes(0, 0)
             replicate(0)
-            x_to_scratch(0, 2, 6)
-            x_to_scratch(0, 6, 8)
-            load_chunk(1, (1,))
-            warm(2)
-            replicate_transposes(0, wk, "wk")
             replicate(1)
+            warm(2, sps[(0, 1)])
+            silu_transposes(0, 1)
+            replicate_transposes(0, accp, "acc")
+            replicate_transposes(1, accp, "acc")
             for g in range(2):
                 silu_quantise(0, g)
-            basis_squares(0)
-            basis_squares(1)
-            load_x4(0, 0)
-            load_chunk(2)
+            for n in range(N_DIRECT):
+                basis_squares(n)
             for s in range(HEAD_STEPS):
                 step(s)
         ostage = ctx.enter_context(tc.tile_pool(name="ostage", bufs=4))
@@ -427,8 +430,7 @@ def tile_kanlinear_kernel(tc, x, base_w, base_b, spline_w, out):
         items = [(n, None) for n in range(N_STEPS, 30)] + [(n, mm) for mm in range(2) for n in (30, 31)]
         for k in range(len(items) + 1):
             if k == 0:
-                for j in (2 * N_STEPS - 2, 2 * N_STEPS - 1):
-                    w_quantise(j)
+                w_quantise(N_STEPS - 1)
             if k + 1 < len(items):
                 basis_squares(*items[k + 1])
             if k + 2 < len(items):
@@ -440,7 +442,7 @@ def tile_kanlinear_kernel(tc, x, base_w, base_b, spline_w, out):
             else:
                 basis_quantise(*items[k - 1])
             if k < MX_LAG:
-                for j in (2 * (N_STEPS + k - MX_LAG), 2 * (N_STEPS + k - MX_LAG) + 1):
+                for j in range(2 * N_STEPS - MX_RUN_LAG + 2 * k, min(2 * N_STEPS, 2 * N_STEPS - MX_RUN_LAG + 2 * k + 2)):
                     mx(accs, j, 0)
             if k == MX_LAG:
                 accs2.update(new_accs(wk, "wk"))

@@ -27,7 +27,8 @@ FLOPS = 2 * ROWS * OUT_F * (IN_F + IN_F * GRID)
 N_STEPS = 18
 HEAD_STEPS = 8
 MX_LAG = 3
-MX_RUN_LAG = 5
+FIRST_MX_BANK = 14
+MX_RUN = 3
 N_CHUNKS = 3
 N_DIRECT = 4
 
@@ -320,6 +321,21 @@ def tile_kanlinear_kernel(tc, x, base_w, base_b, spline_w, out):
             for mm in range(2):
                 mx_one(accs, kk, half, mm, r)
 
+        fills = []
+        passes = []
+
+        def mx_group(n):
+            for i in range(len(passes), len(passes) + n):
+                mx_one(accs, units[i // 2][0], units[i // 2][1], i % 2, 0)
+                passes.append(i)
+
+        def after_fill():
+            if not fills:
+                accs.update(new_accs(accp, "acc"))
+            if len(fills) % MX_RUN == 0:
+                mx_group(MX_RUN)
+            fills.append(1)
+
         def new_accs(pool, tag):
             accs = {}
             for half in range(2):
@@ -335,7 +351,7 @@ def tile_kanlinear_kernel(tc, x, base_w, base_b, spline_w, out):
             nc.sync.dma_start(out=of[r0 : r0 + P, cols], in_=res[:])
 
         accs = {}
-        WARM = {0: 2, 1: 2, 2: 2, 3: 2, 4: 2, 5: 2}
+        WARM = {0: 2, 2: 2, 4: 2, 6: 2, 8: 2, 10: 2, 12: 2, 18: 2}
 
         def warm(count, bank):
             for i in range(count):
@@ -344,17 +360,15 @@ def tile_kanlinear_kernel(tc, x, base_w, base_b, spline_w, out):
         def step(s):
             pair = (2 * s, 2 * s + 1)
             for q in range(2):
-                run = 2 * s + q
-                if run == MX_RUN_LAG:
-                    accs.update(new_accs(accp, "acc"))
                 for j in pair:
-                    w_transposes(j, q, WARM.get(run, 0) if j == 2 * s else 0)
-                if run == 2:
-                    for g in range(2):
-                        silu_bank(1, g)
-                        silu_transposes(1, g)
-                if run >= MX_RUN_LAG:
-                    mx(accs, run - MX_RUN_LAG, 0)
+                    bank = 4 * s + 2 * q + j % 2
+                    w_transposes(j, q, WARM.get(bank, 0))
+                    if bank == 5:
+                        for g in range(2):
+                            silu_bank(1, g)
+                            silu_transposes(1, g)
+                    if bank >= FIRST_MX_BANK:
+                        after_fill()
             for j in pair:
                 w_evict(j, 0)
             if s >= 1:
@@ -385,10 +399,9 @@ def tile_kanlinear_kernel(tc, x, base_w, base_b, spline_w, out):
                 load_x4(1, (10, 15).index(s))
             if s == 16:
                 nc.sync.dma_start(out=bias_bc[:], in_=base_b.partition_broadcast(P))
-            if s == 5:
-                x_to_scratch(1, 0, 4)
-            if s == 6:
-                x_to_scratch(1, 4, 8)
+            if s in (5, 6):
+                x_to_scratch(1, 4 * (s - 5), 4 * (s - 5) + 4)
+                after_fill()
             if s == 2:
                 basis_quantise(0)
             if s >= 2:
@@ -441,20 +454,20 @@ def tile_kanlinear_kernel(tc, x, base_w, base_b, spline_w, out):
                 basis_quantise(N_STEPS - 1)
             else:
                 basis_quantise(*items[k - 1])
-            if k < MX_LAG:
-                for j in range(2 * N_STEPS - MX_RUN_LAG + 2 * k, min(2 * N_STEPS, 2 * N_STEPS - MX_RUN_LAG + 2 * k + 2)):
-                    mx(accs, j, 0)
-            if k == MX_LAG:
+            if k == 0:
+                mx_group(4 * N_STEPS - 4 - len(passes))
                 accs2.update(new_accs(wk, "wk"))
                 for j in range(4):
                     mx(accs2, j, 1)
-                for n in range(16, N_STEPS + k - 1):
+            if k == 1:
+                mx_group(4)
+                for n in range(16, N_STEPS):
                     for half in range(2):
                         for mm in range(2):
                             mx_one(accs2, ("s", n - 16), half, mm, 1)
-            if MX_LAG <= k < MX_LAG + 4:
-                finish(accs, 0, (k - MX_LAG) // 2, (k - MX_LAG) % 2)
-            if k >= MX_LAG:
+            if 3 <= k < 3 + 4:
+                finish(accs, 0, (k - 3) // 2, (k - 3) % 2)
+            if k >= 1:
                 n, part = items[k - 1]
                 if part is None:
                     for half in range(2):

@@ -34,7 +34,7 @@ N_DIRECT = 4
 
 
 def act_evicts(s, b):
-    return s >= 2 and (b == 1 or (b == 3 and s < 12 and s % 2 == 1))
+    return s >= 2 and (b == 2 or (b == 3 and s < 12 and s % 2 == 1))
 
 
 def vector_squares(n):
@@ -124,7 +124,7 @@ def tile_kanlinear_kernel(tc, x, base_w, base_b, spline_w, out):
         neg_mid_e = [per_partition("neg_mid%d" % e, -STEP, 2.0 - STEP / 2 + (STEP, -STEP)[e]) for e in range(2)]
         exp_bias = per_partition("exp_bias", 0.0, -CINV * CINV * STEP * STEP / 4)
 
-        def x_to_scratch(r, j0, j1):
+        def x_transposes(r, j0, j1):
             xp = wk.tile([P, 1024], BF16, tag="wk", name="xp")
             for jt in range(j0, j1):
                 for mm in range(2):
@@ -134,9 +134,20 @@ def tile_kanlinear_kernel(tc, x, base_w, base_b, spline_w, out):
                         in_=x_nat[:, c0 : c0 + P],
                         identity=ident_b[:],
                     )
+            return xp
+
+        def x_copy(xp, n):
             xt = head.tile([P, 1024], BF16, tag="xt", bufs=2, name="xt")
-            nc.vector.tensor_copy(out=xt[:, 0 : 256 * (j1 - j0)], in_=xp[:, 0 : 256 * (j1 - j0)])
+            nc.vector.tensor_copy(out=xt[:, 0 : 256 * n], in_=xp[:, 0 : 256 * n])
+            return xt
+
+        def x_store(xt, r, j0, j1):
             nc.sync.dma_start(out=scr[r][:, P * j0 : P * j1], in_=xt[:].bitcast(F32)[:, 0 : P * (j1 - j0)])
+
+        def x_to_scratch(r, j0, j1):
+            x_store(x_copy(x_transposes(r, j0, j1), j1 - j0), r, j0, j1)
+
+        x_early = []
 
         reps = {}
         xreps = {}
@@ -351,7 +362,7 @@ def tile_kanlinear_kernel(tc, x, base_w, base_b, spline_w, out):
             nc.sync.dma_start(out=of[r0 : r0 + P, cols], in_=res[:])
 
         accs = {}
-        WARM = {0: 2, 2: 2, 4: 2, 6: 2, 8: 2, 10: 2, 12: 2, 18: 2}
+        WARM = {0: 2, 2: 2, 4: 2, 6: 2, 8: 2, 10: 2, 12: 2}
 
         def warm(count, bank):
             for i in range(count):
@@ -369,12 +380,18 @@ def tile_kanlinear_kernel(tc, x, base_w, base_b, spline_w, out):
                             silu_transposes(1, g)
                     if bank >= FIRST_MX_BANK:
                         after_fill()
+                    if bank == 9:
+                        for i in range(2):
+                            x_early.append(x_transposes(1, 4 * i, 4 * i + 4))
             for j in pair:
                 w_evict(j, 0)
             if s >= 1:
                 w_quantise(s - 1)
             if s >= 3:
                 basis_squares(s + 1)
+            if s == 2:
+                for i in range(2):
+                    x_early[i] = x_copy(x_early[i], 4)
             for j in pair:
                 w_evict(j, 1)
             if s == 1:
@@ -399,9 +416,8 @@ def tile_kanlinear_kernel(tc, x, base_w, base_b, spline_w, out):
                 load_x4(1, (10, 15).index(s))
             if s == 16:
                 nc.sync.dma_start(out=bias_bc[:], in_=base_b.partition_broadcast(P))
-            if s in (5, 6):
-                x_to_scratch(1, 4 * (s - 5), 4 * (s - 5) + 4)
-                after_fill()
+            if s in (6, 7):
+                x_store(x_early[s - 6], 1, 4 * (s - 6), 4 * (s - 6) + 4)
             if s == 2:
                 basis_quantise(0)
             if s >= 2:

@@ -34,7 +34,7 @@ N_DIRECT = 4
 
 
 def act_evicts(s, b):
-    return s >= 2 and (b == 2 or (b == 3 and s < 12 and s % 2 == 1))
+    return s >= 2 and (b == 2 or (b == 3 and s < 14 and s % 2 == 1))
 
 
 def vector_squares(n):
@@ -154,13 +154,17 @@ def tile_kanlinear_kernel(tc, x, base_w, base_b, spline_w, out):
 
         def replicate(pair):
             rp = head.tile([P, 1024], BF16, tag="rep", bufs=2, name="rep")
-            nc.vector.tensor_copy(
-                out=rp[:].rearrange("p (m f s) -> p m f s", m=2, s=4),
-                in_=x_nat[:]
+            dst = rp[:].rearrange("p (m f s) -> p m f s", m=2, s=4)
+            src = (
+                x_nat[:]
                 .rearrange("p (m i) -> p m i", m=4)[:, 0:2, P * pair : P * pair + P]
                 .unsqueeze(3)
-                .to_broadcast([P, 2, P, 4]),
+                .to_broadcast([P, 2, P, 4])
             )
+            if pair == 0:
+                nc.vector.tensor_copy(out=dst, in_=src)
+            else:
+                nc.gpsimd.tensor_scalar(out=dst, in0=src, scalar1=1.0, scalar2=0.0, op0=ALU.mult, op1=ALU.add)
             reps[pair] = rp
 
         def replicate_transposes(pair, pool, tag):
@@ -481,8 +485,8 @@ def tile_kanlinear_kernel(tc, x, base_w, base_b, spline_w, out):
                     for half in range(2):
                         for mm in range(2):
                             mx_one(accs2, ("s", n - 16), half, mm, 1)
-            if 3 <= k < 3 + 4:
-                finish(accs, 0, (k - 3) // 2, (k - 3) % 2)
+            if k in (2, 5, 8, 11):
+                finish(accs, 0, (2, 5, 8, 11).index(k) // 2, (2, 5, 8, 11).index(k) % 2)
             if k >= 1:
                 n, part = items[k - 1]
                 if part is None:

from contextlib import ExitStack

import concourse.mybir as mybir
from concourse.masks import make_identity

F32 = mybir.dt.float32
BF16 = mybir.dt.bfloat16
U32 = mybir.dt.uint32
U8 = mybir.dt.uint8
FP8X4 = mybir.dt.float8_e4m3fn_x4
ACT = mybir.ActivationFunctionType
ALU = mybir.AluOpType
AX = mybir.AxisListType

P = 128
ROWS = 512
IN_F = 1024
OUT_F = 1024
GRID = 8
HALF = 512
RH = 256
STEP = 4.0 / 7.0
CINV = 1.0 / (STEP + 1e-06)

FLOPS = 2 * ROWS * OUT_F * (IN_F + IN_F * GRID)

N_STEPS = 18
HEAD_STEPS = 8
MX_LAG = 3
FIRST_MX_BANK = 14
MX_RUN = 3
N_CHUNKS = 3
N_DIRECT = 4


def act_evicts(s, b):
    return s >= 2 and (b == 2 or (b == 3 and s < 14 and s % 2 == 1))


def vector_squares(n):
    return n >= 20 and n % 3 != 0


def tile_kanlinear_kernel(tc, x, base_w, base_b, spline_w, out):
    nc = tc.nc
    xf = x.flatten_outer_dims()
    of = out.flatten_outer_dims()
    sw = spline_w.rearrange("o i g -> o (i g)")
    scr = [of[384:512, :], of[256:384, :]]

    with ExitStack() as ctx:
        ctx.enter_context(tc.manual_schedule())
        const = ctx.enter_context(tc.tile_pool(name="const", bufs=1))
        keep = ctx.enter_context(tc.tile_pool(name="keep", bufs=1))
        chunks = ctx.enter_context(tc.tile_pool(name="chunks", bufs=N_CHUNKS))
        wgrps = ctx.enter_context(tc.tile_pool(name="wgrps", bufs=2))
        x4p = ctx.enter_context(tc.tile_pool(name="x4p", bufs=2))
        qpool = ctx.enter_context(tc.tile_pool(name="qpool", bufs=4))
        mids = ctx.enter_context(tc.tile_pool(name="mids", bufs=2))
        bgrps = ctx.enter_context(tc.tile_pool(name="bgrps", bufs=3))
        accp = ctx.enter_context(tc.psum_pool(name="accp", bufs=4))
        wk = ctx.enter_context(tc.psum_pool(name="wk", bufs=4))

        chunk_of = {}
        chunk_words = {}

        def load_chunk(i, parts=(0, 1)):
            if i not in chunk_of:
                chunk_of[i] = chunks.tile([P, 8192], BF16, tag="chunk", name="chunk%d" % i)
            ch = chunk_of[i]
            region, half = divmod(i - 1, 2)
            src = base_w if i == 0 else sw[HALF * half : HALF * half + HALF, 2048 * region : 2048 * region + 2048]
            for part in parts:
                width = 2048 if i == 0 else 4096
                nc.sync.dma_start(
                    out=ch[:, width * part : width * part + width].rearrange("p (n k) -> p n k", n=2),
                    in_=src[2 * P * part : 2 * P * part + 2 * P, :].rearrange("(n p) k -> p n k", p=P),
                )
            chunk_words[i] = ch[:].bitcast(F32)

        def load_x(r, cols):
            nc.sync.dma_start(
                out=x_nat[:, 2048 * r : 2048 * r + 2048].rearrange("p (m i) -> p m i", m=2)[:, :, cols],
                in_=xf[RH * r : RH * r + RH, cols].rearrange("(m p) i -> p m i", p=P),
            )

        x4s = {}

        def load_x4(r, h):
            t = x4p.tile([P, 4096], BF16, tag="x4", name="x4_%d_%d" % (r, h))
            tw = t[:].bitcast(F32).rearrange("p (d w) -> p d w", d=4)
            w0 = 256 if (r, h) == (0, 0) else 0
            for s in range(4):
                nc.sync.dma_start(
                    out=tw[s:P:4, :, w0:512],
                    in_=scr[r][:, 512 * h + w0 : 512 * h + 512].rearrange("(d q) w -> q d w", q=32),
                )
            x4s[(r, h)] = t

        acts = {}
        ident_f = const.tile([P, P], F32)
        ident_b = const.tile([P, P], BF16)
        zeros = const.tile([P, HALF], BF16)
        table_in = const.tile([P, 1], F32)
        table_out = const.tile([P, 1], F32)
        nc.vector.memset(zeros[:], 0.0)
        nc.vector.memset(table_in[:], 0.0)
        make_identity(nc, ident_b[:])
        make_identity(nc, ident_f[:])
        vals = const.tile([P, P], F32)
        for q in range(4):
            nc.vector.memset(vals[:].rearrange("p (f s) -> p f s", s=4)[:, :, q], float(2 * q))
        nc.vector.tensor_tensor(out=vals[:], in0=vals[:], in1=ident_f[:], op=ALU.mult)
        index2 = const.tile([P, 1], F32)
        nc.vector.reduce_sum(out=index2[:], in_=vals[:], axis=AX.X)

        def per_partition(name, mul, add):
            t = const.tile([P, 1], F32, name=name)
            nc.vector.tensor_scalar(out=t[:], in0=index2[:], scalar1=mul, scalar2=add, op0=ALU.mult, op1=ALU.add)
            return t

        sq_bias = [per_partition("sq_bias%d" % e, -CINV * STEP, CINV * (2.0 - STEP * e)) for e in range(2)]
        neg_mid = per_partition("neg_mid", -STEP, 2.0 - STEP / 2)
        neg_mid_e = [per_partition("neg_mid%d" % e, -STEP, 2.0 - STEP / 2 + (STEP, -STEP)[e]) for e in range(2)]
        exp_bias = per_partition("exp_bias", 0.0, -CINV * CINV * STEP * STEP / 4)

        def x_transposes(r, j0, j1):
            xp = wk.tile([P, 1024], BF16, tag="wk", name="xp")
            for jt in range(j0, j1):
                for mm in range(2):
                    c0 = IN_F * (2 * r + mm) + P * jt
                    nc.tensor.transpose(
                        out=xp[:, 256 * (jt - j0) + P * mm : 256 * (jt - j0) + P * mm + P],
                        in_=x_nat[:, c0 : c0 + P],
                        identity=ident_b[:],
                    )
            return xp

        def x_copy(xp, n):
            xt = head.tile([P, 1024], BF16, tag="xt", bufs=2, name="xt")
            nc.vector.tensor_copy(out=xt[:, 0 : 256 * n], in_=xp[:, 0 : 256 * n])
            return xt

        def x_store(xt, r, j0, j1):
            nc.sync.dma_start(out=scr[r][:, P * j0 : P * j1], in_=xt[:].bitcast(F32)[:, 0 : P * (j1 - j0)])

        def x_to_scratch(r, j0, j1):
            x_store(x_copy(x_transposes(r, j0, j1), j1 - j0), r, j0, j1)

        x_early = []

        reps = {}
        xreps = {}

        def replicate(pair):
            rp = head.tile([P, 1024], BF16, tag="rep", bufs=2, name="rep")
            dst = rp[:].rearrange("p (m f s) -> p m f s", m=2, s=4)
            src = (
                x_nat[:]
                .rearrange("p (m i) -> p m i", m=4)[:, 0:2, P * pair : P * pair + P]
                .unsqueeze(3)
                .to_broadcast([P, 2, P, 4])
            )
            if pair == 0:
                nc.vector.tensor_copy(out=dst, in_=src)
            else:
                nc.gpsimd.tensor_scalar(out=dst, in0=src, scalar1=1.0, scalar2=0.0, op0=ALU.mult, op1=ALU.add)
            reps[pair] = rp

        def replicate_transposes(pair, pool, tag):
            xr = pool.tile([P, 1024], BF16, tag=tag, name="xr")
            for v in range(4):
                for mm in range(2):
                    c0 = 512 * mm + P * v
                    nc.tensor.transpose(
                        out=xr[:, 256 * v + P * mm : 256 * v + P * mm + P],
                        in_=reps[pair][:, c0 : c0 + P],
                        identity=ident_b[:],
                    )
            xreps[pair] = xr

        sgrps = {}
        sps = {}

        def silu_bank(r, g):
            sps[(r, g)] = accp.tile([P, 512], F32, tag="acc", name="sp")

        def silu_transposes(r, g):
            x_words = x_nat[:].bitcast(F32)
            sp = sps[(r, g)]
            for u in range(2):
                for mm in range(2):
                    c0 = 512 * (2 * r + mm) + 256 * g + P * u
                    nc.tensor.transpose(
                        out=sp[:, 256 * u + P * mm : 256 * u + P * mm + P],
                        in_=x_words[:, c0 : c0 + P],
                        identity=ident_f[:],
                    )
            grp = head.tile([P, 4 * RH], BF16, align_bytes=64, tag="sgrp", bufs=2, name="sgrp")
            nc.scalar.activation(
                out=grp[:].rearrange("p (r u e) -> p r u e", u=2, e=2),
                in_=sp[:].bitcast(BF16).rearrange("p (u r e) -> p r u e", u=2, e=2),
                func=ACT.Silu,
            )
            sgrps[(r, g)] = grp

        def silu_quantise(r, g):
            codes = keep.tile([P, RH], U32, align_bytes=64, name="sq_%d_%d" % (r, g))
            plane = keep.tile([P, RH], U8, align_bytes=64, name="ss_%d_%d" % (r, g))
            nc.vector.quantize_mx(out=codes[:].bitcast(FP8X4), scales=plane[:], in_=sgrps[(r, g)][:])
            for mm in range(2):
                acts[(("b", g), r, mm)] = (codes, plane, P * mm)

        units = [(("b", g), half, 0) for half in range(2) for g in range(2)]
        units += [(("s", 4 * i + b), half, 1 + 2 * i + half) for i in range(4) for half in range(2) for b in range(4)]
        wgrp_of = {}
        banks = {}
        wts = {}

        def w_transposes(j, q, n_warm=0):
            kk, half, ci = units[j]
            wt = wk.tile([P, 512], F32, tag="wk", name="wt")
            warm(n_warm, wt)
            for nn in range(2):
                for u in range(2):
                    n = 2 * q + nn
                    c0 = (512 * (4 * half + n) if ci == 0 else 1024 * n) + 256 * kk[1] % 1024 + P * u
                    nc.tensor.transpose(
                        out=wt[:, 256 * nn + P * u : 256 * nn + P * u + P],
                        in_=chunk_words[ci][:, c0 : c0 + P],
                        identity=ident_f[:],
                    )
            banks[(j, q)] = wt

        def w_evict(j, q):
            if j % 2 == 0 and q == 0:
                wgrp_of[j // 2] = wgrps.tile([P, 8 * HALF], BF16, align_bytes=64, tag="wgrp", name="wgrp")
            c0 = 1024 * (j % 2) + 512 * q
            dst = wgrp_of[j // 2][:].bitcast(F32)[:, c0 : c0 + 512].rearrange("p (n o u) -> p n o u", n=2, u=2)
            srcv = banks[(j, q)][:].rearrange("p (n u o) -> p n o u", n=2, u=2)
            if act_evicts(j // 2, 2 * q + j % 2):
                nc.scalar.copy(out=dst, in_=srcv)
            else:
                nc.vector.tensor_copy(out=dst, in_=srcv)

        def w_quantise(s):
            codes = keep.tile([P, 2 * HALF], U32, align_bytes=64, name="wq_%d" % s)
            plane = keep.tile([P, 2 * HALF], U8, align_bytes=64, name="ws_%d" % s)
            nc.vector.quantize_mx(out=codes[:].bitcast(FP8X4), scales=plane[:], in_=wgrp_of[s][:])
            for i in range(2):
                kk, half, ci = units[2 * s + i]
                cols = slice(HALF * i, HALF * i + HALF)
                wts[(kk, half)] = (codes[:, cols], plane[:, cols])

        grp_of = {}
        qq_of = {}

        mid_of = {}

        def basis_x(n, mm):
            r, c = divmod(n, 16)
            if n < N_DIRECT:
                return xreps[c // 2][:].rearrange("p (v r) -> p v r", v=4)[:, 2 * (c % 2) : 2 * (c % 2) + 2, :]
            x4 = x4s[(r, c // 8)][:].rearrange("p (d t r) -> p d t r", d=4, t=4)
            rows = slice(0, RH) if mm is None else slice(P * mm, P * mm + P)
            return x4[:, 2 * (c % 2) : 2 * (c % 2) + 2, c // 2 % 4, rows]

        def n_rows(mm):
            return RH if mm is None else P

        def basis_mid(n, mm=None):
            if vector_squares(n):
                mid = mids.tile([P, 2 * RH], F32, tag="mid", name="mid")
                nc.vector.tensor_scalar(
                    out=mid[:, 0 : 2 * n_rows(mm)].rearrange("p (u r) -> p u r", u=2),
                    in0=basis_x(n, mm),
                    scalar1=neg_mid[:, 0:1],
                    scalar2=None,
                    op0=ALU.add,
                )
                mid_of[(n, mm)] = mid

        def basis_squares(n, mm=None):
            src = basis_x(n, mm)
            qq = qpool.tile([P, 4 * RH], F32, tag="qq", name="qq")
            qv = qq[:, 0 : 4 * n_rows(mm)].rearrange("p (u e r) -> p u e r", u=2, e=2)
            if vector_squares(n):
                mv = mid_of[(n, mm)][:, 0 : 2 * n_rows(mm)].rearrange("p (u r) -> p u r", u=2)
                for e in range(2):
                    nc.vector.scalar_tensor_tensor(
                        out=qv[:, :, e, :], in0=src, scalar=neg_mid_e[e][:, 0:1], in1=mv, op0=ALU.add, op1=ALU.mult
                    )
            else:
                for e in range(2):
                    nc.scalar.activation(
                        out=qv[:, :, e, :], in_=src, func=ACT.Square, bias=sq_bias[e][:, 0:1], scale=CINV
                    )
            qq_of[(n, mm)] = qq

        def basis_exp(n, mm=None):
            grp = bgrps.tile([P, 4 * RH], BF16, align_bytes=64, tag="bgrp", name="bgrp")
            width = 4 * n_rows(mm)
            dst = grp[:, 0:width].rearrange("p (c i t) -> p c t i", i=4, t=4)
            srcv = qq_of[(n, mm)][:, 0:width].rearrange("p (t c i) -> p c t i", i=4, t=4)
            if vector_squares(n):
                nc.scalar.activation(out=dst, in_=srcv, func=ACT.Exp, bias=exp_bias[:, 0:1], scale=-CINV * CINV)
            else:
                nc.scalar.activation(out=dst, in_=srcv, func=ACT.Exp, scale=-1.0)
            grp_of[(n, mm)] = grp

        def basis_quantise(n, mm=None):
            w = n_rows(mm)
            codes = bcp.tile([P, RH], U32, align_bytes=64, tag="codes", name="bq")
            plane = bcp.tile([P, RH], U8, align_bytes=64, tag="plane", name="bs")
            nc.vector.quantize_mx(
                out=codes[:, 0:w].bitcast(FP8X4), scales=plane[:, 0:w], in_=grp_of[(n, mm)][:, 0 : 4 * w]
            )
            for i in range(w // P):
                acts[(("s", n % 16), n // 16, mm or i)] = (codes, plane, P * i)

        def mx_one(accs, kk, half, mm, r):
            a_c, a_p, r0 = acts[(kk, r, mm)]
            w_c, w_p = wts[(kk, half)]
            nc.tensor.matmul_mx(
                out=accs[(mm, half)][:],
                lhsT=a_c[:, r0 : r0 + P].bitcast(FP8X4),
                lhsT_scale=a_p[:, r0 : r0 + P],
                rhs=w_c.bitcast(FP8X4),
                rhs_scale=w_p,
                start=(kk == ("b", 0)),
                stop=(kk == ("s", 15)),
            )

        def mx(accs, j, r):
            kk, half, ci = units[j]
            for mm in range(2):
                mx_one(accs, kk, half, mm, r)

        fills = []
        passes = []

        def mx_group(n):
            for i in range(len(passes), len(passes) + n):
                mx_one(accs, units[i // 2][0], units[i // 2][1], i % 2, 0)
                passes.append(i)

        def after_fill():
            if not fills:
                accs.update(new_accs(accp, "acc"))
            if len(fills) % MX_RUN == 0:
                mx_group(MX_RUN)
            fills.append(1)

        def new_accs(pool, tag):
            accs = {}
            for half in range(2):
                for mm in range(2):
                    accs[(mm, half)] = pool.tile([P, HALF], F32, tag=tag, name="acc%d%d" % (mm, half))
            return accs

        def finish(accs, r, half, mm):
            cols = slice(HALF * half, HALF * half + HALF)
            res = ostage.tile([P, HALF], F32, tag="res", name="res")
            nc.vector.tensor_tensor(out=res[:], in0=accs[(mm, half)][:], in1=bias_bc[:, cols], op=ALU.add)
            r0 = RH * r + P * mm
            nc.sync.dma_start(out=of[r0 : r0 + P, cols], in_=res[:])

        accs = {}
        WARM = {0: 2, 2: 2, 4: 2, 6: 2, 8: 2, 10: 2, 12: 2}

        def warm(count, bank):
            for i in range(count):
                nc.tensor.matmul(out=bank[:], lhsT=zeros[:, 0:P], rhs=zeros[:], start=True, stop=True)

        def step(s):
            pair = (2 * s, 2 * s + 1)
            for q in range(2):
                for j in pair:
                    bank = 4 * s + 2 * q + j % 2
                    w_transposes(j, q, WARM.get(bank, 0))
                    if bank == 5:
                        for g in range(2):
                            silu_bank(1, g)
                            silu_transposes(1, g)
                    if bank >= FIRST_MX_BANK:
                        after_fill()
                    if bank == 9:
                        for i in range(2):
                            x_early.append(x_transposes(1, 4 * i, 4 * i + 4))
            for j in pair:
                w_evict(j, 0)
            if s >= 1:
                w_quantise(s - 1)
            if s >= 3:
                basis_squares(s + 1)
            if s == 2:
                for i in range(2):
                    x_early[i] = x_copy(x_early[i], 4)
            for j in pair:
                w_evict(j, 1)
            if s == 1:
                basis_exp(0)
            if s >= 1:
                basis_exp(s)
            if s == 0:
                x_to_scratch(0, 2, 6)
                load_chunk(1, (1,))
            if s == 0:
                x_to_scratch(0, 6, 8)
                load_x4(0, 0)
                load_chunk(2)
            if s == 4:
                for g in range(2):
                    silu_quantise(1, g)
            if s == 3:
                load_x4(0, 1)
            if s % 2 == 1 and s // 2 + N_CHUNKS < 9:
                load_chunk(s // 2 + N_CHUNKS)
            if s in (10, 15):
                load_x4(1, (10, 15).index(s))
            if s == 16:
                nc.sync.dma_start(out=bias_bc[:], in_=base_b.partition_broadcast(P))
            if s in (6, 7):
                x_store(x_early[s - 6], 1, 4 * (s - 6), 4 * (s - 6) + 4)
            if s == 2:
                basis_quantise(0)
            if s >= 2:
                basis_quantise(s - 1)

        bcp = ctx.enter_context(tc.tile_pool(name="bcp", bufs=9))
        with tc.tile_pool(name="head", bufs=1) as head:
            x_nat = head.tile([P, 4 * IN_F], BF16)
            for g in range(2):
                load_x(0, slice(512 * g, 512 * g + 512))
            load_chunk(0, range(3))
            load_x(1, slice(0, IN_F))
            load_chunk(0, range(3, 4))
            load_chunk(1, (0,))
            nc.scalar.activation(out=table_out[:], in_=table_in[:], func=ACT.Silu)
            for g in range(2):
                silu_bank(0, g)
            warm(3, sps[(0, 0)])
            silu_transposes(0, 0)
            replicate(0)
            replicate(1)
            warm(2, sps[(0, 1)])
            silu_transposes(0, 1)
            replicate_transposes(0, accp, "acc")
            replicate_transposes(1, accp, "acc")
            for g in range(2):
                silu_quantise(0, g)
            for n in range(N_DIRECT):
                basis_squares(n)
            for s in range(HEAD_STEPS):
                step(s)
        ostage = ctx.enter_context(tc.tile_pool(name="ostage", bufs=4))
        late = ctx.enter_context(tc.tile_pool(name="late", bufs=1))
        bias_bc = late.tile([P, OUT_F], BF16)
        for s in range(HEAD_STEPS, N_STEPS):
            step(s)

        accs2 = {}
        items = [(n, None) for n in range(N_STEPS, 30)] + [(n, mm) for mm in range(2) for n in (30, 31)]
        for k in range(len(items) + 1):
            if k == 0:
                w_quantise(N_STEPS - 1)
            if k + 1 < len(items):
                basis_squares(*items[k + 1])
            if k + 2 < len(items):
                basis_mid(*items[k + 2])
            if k < len(items):
                basis_exp(*items[k])
            if k == 0:
                basis_quantise(N_STEPS - 1)
            else:
                basis_quantise(*items[k - 1])
            if k == 0:
                mx_group(4 * N_STEPS - 4 - len(passes))
                accs2.update(new_accs(wk, "wk"))
                for j in range(4):
                    mx(accs2, j, 1)
            if k == 1:
                mx_group(4)
                for n in range(16, N_STEPS):
                    for half in range(2):
                        for mm in range(2):
                            mx_one(accs2, ("s", n - 16), half, mm, 1)
            if k in (2, 5, 8, 11):
                finish(accs, 0, (2, 5, 8, 11).index(k) // 2, (2, 5, 8, 11).index(k) % 2)
            if k >= 1:
                n, part = items[k - 1]
                if part is None:
                    for half in range(2):
                        for mm in range(2):
                            mx_one(accs2, ("s", n - 16), half, mm, 1)
                elif n == 31:
                    for half in range(2):
                        for c in (14, 15):
                            mx_one(accs2, ("s", c), half, part, 1)
        for mm in range(2):
            for half in range(2):
                finish(accs2, 1, half, mm)
